import numpy as np
import ml_dtypes


def mxq(x, axis, fmt="e4m3"):
    dtype, down = {"e4m3": (ml_dtypes.float8_e4m3fn, 7), "e5m2": (ml_dtypes.float8_e5m2, 14)}[fmt]
    v = np.moveaxis(np.asarray(x, np.float32).astype(ml_dtypes.bfloat16).astype(np.float64), axis, -1)
    blocks = v.reshape(v.shape[:-1] + (-1, 32))
    amax = np.abs(blocks).max(-1, keepdims=True)
    byte = np.maximum(np.where(amax > 0, np.frexp(amax)[1] - 1 + 127, 0) - down, 1)
    scale = np.exp2(byte - 127.0)
    codes = (blocks / scale).astype(np.float32).astype(dtype).astype(np.float64)
    return np.moveaxis((codes * scale).reshape(v.shape), -1, axis)


WIDE = False


def mx_kscale(k):
    if not WIDE:
        return np.ones(k)
    levels = np.array([10, -10, 5, -5, 0])
    a = np.random.permutation(np.resize(levels, k // 512 * 4)).reshape(k // 512, 4)
    idx = np.arange(k)
    return np.exp2(a[idx // 512, idx % 128 // 32])


BF16 = ml_dtypes.bfloat16


def bf(x):
    return np.asarray(x, np.float32).astype(BF16)


def f64(x):
    return np.asarray(x).astype(np.float64)


E2M1 = np.array([0.0, 0.5, 1.0, 1.5, 2.0, 3.0, 4.0, 6.0, -0.0, -0.5, -1.0, -1.5, -2.0, -3.0, -4.0, -6.0])


def pack_weight(w, fmt):
    k, n = w.shape
    w = f64(bf(w)).reshape(k // 32, 32, n)
    amax = np.abs(w).max(1)
    if fmt == "e4m3":
        byte = np.frexp(amax)[1] - 1 + 127 - 7
    else:
        mant, ex = np.frexp(amax / 6.0)
        byte = np.where(mant > 0.5, ex, ex - 1) + 127
    byte = np.clip(np.where(amax > 0, byte, 1), 1, 254)
    scaled = (w * np.exp2(127.0 - byte)[:, None, :]).reshape(k, n).astype(np.float32)
    by_word = np.ascontiguousarray(scaled.reshape(k // 512, 128, 4, n).transpose(0, 1, 3, 2))
    if fmt == "e4m3":
        words = by_word.astype(ml_dtypes.float8_e4m3fn).view(np.uint8)
    else:
        c = by_word.astype(ml_dtypes.float4_e2m1fn).view(np.uint8) & 0xF
        words = c[..., 0::2] | (c[..., 1::2] << 4)
    return np.ascontiguousarray(words), np.ascontiguousarray(byte.astype(np.uint8).reshape(k // 512, 16, n))


def unpack_weight(words, scales, fmt):
    g, p, n, _ = words.shape
    if fmt == "e4m3":
        vals = np.ascontiguousarray(words).view(ml_dtypes.float8_e4m3fn).astype(np.float64)
    else:
        nib = np.empty((g, p, n, 4), np.uint8)
        nib[..., 0::2] = words & 0xF
        nib[..., 1::2] = words >> 4
        vals = E2M1[nib]
    vals = vals * np.repeat(np.exp2(scales.astype(np.float64) - 127.0), 8, axis=1)[..., None]
    return vals.transpose(0, 1, 3, 2).reshape(g * 512, n)


B, N, NF, ND, NH = 4, 32, 512, 1024, 512


def setup_inputs():
    s = mx_kscale(ND)
    t = mx_kscale(NH)
    atom_features = bf(np.random.standard_normal((B, N, NF)))
    distance_matrix = bf(np.random.random((B, N, N, ND)) * s)
    distance_matrix_mask = bf(0.25 + 0.75 * np.random.random((B, N, N)))
    W_cf = bf(np.random.standard_normal((NF, NH)) / np.sqrt(NF) * t)
    W_df_words, W_df_scales = pack_weight(np.random.standard_normal((ND, NH)) * 1.5 / np.sqrt(ND) / s[:, None], "e4m3")
    W_fc_words, W_fc_scales = pack_weight(np.random.standard_normal((NH, NF)) / np.sqrt(NH) / t[:, None], "e4m3")
    b_cf = bf(np.random.standard_normal(NH) * 0.3 * t)
    b_df = bf(np.random.standard_normal(NH) * 0.3)
    return {
        "atom_features": atom_features,
        "distance_matrix": distance_matrix,
        "distance_matrix_mask": distance_matrix_mask,
        "W_cf": W_cf,
        "W_df_words": W_df_words,
        "W_df_scales": W_df_scales,
        "W_fc_words": W_fc_words,
        "W_fc_scales": W_fc_scales,
        "b_cf": b_cf,
        "b_df": b_df,
    }


def reference(atom_features, distance_matrix, distance_matrix_mask, W_cf, W_df_words, W_df_scales, W_fc_words, W_fc_scales, b_cf, b_df):
    a = f64(atom_features)
    dist_h = (mxq(f64(distance_matrix), 3, "e4m3") @ unpack_weight(W_df_words, W_df_scales, "e4m3")) + f64(b_df)
    atom_h = a @ f64(W_cf) + f64(b_cf)
    gated = dist_h * atom_h[:, None, :, :]
    out = mxq(gated, 3, "e4m3") @ unpack_weight(W_fc_words, W_fc_scales, "e4m3")
    out = out * f64(distance_matrix_mask)[..., None]
    return np.tanh(out).sum(axis=2) + a

@@ -1,0 +1,269 @@
+from contextlib import ExitStack
+
+import concourse.mybir as mybir
+from concourse.masks import make_identity
+
+F32 = mybir.dt.float32
+BF16 = mybir.dt.bfloat16
+I32 = mybir.dt.int32
+U32 = mybir.dt.uint32
+U8 = mybir.dt.uint8
+FP8X4 = mybir.dt.float8_e4m3fn_x4
+ADD = mybir.AluOpType.add
+MULT = mybir.AluOpType.mult
+TANH = mybir.ActivationFunctionType.Tanh
+
+P = 128
+PACK = 4
+MOLS = 4
+ATOMS = 32
+NF = 512
+ND = 1024
+NH = 512
+D_PASSES = ND // (P * PACK)
+F_CHUNKS = NF // P
+SET = 2
+SETS = ATOMS // SET
+
+FLOPS = 2 * MOLS * ATOMS * ATOMS * (ND * NH + NH * NF) + 2 * MOLS * ATOMS * NF * NH
+
+
+def tile_dtnnstep_pa_kernel(
+    tc,
+    atom_features,
+    distance_matrix,
+    distance_matrix_mask,
+    W_cf,
+    W_df_words,
+    W_df_scales,
+    W_fc_words,
+    W_fc_scales,
+    b_cf,
+    b_df,
+    out,
+):
+    nc = tc.nc
+    with ExitStack() as stack:
+        stack.enter_context(tc.manual_schedule())
+        consts = stack.enter_context(tc.tile_pool(name="consts", bufs=1))
+        d_pool = stack.enter_context(tc.tile_pool(name="d_pool", bufs=SETS))
+        work = stack.enter_context(tc.tile_pool(name="work", bufs=2))
+        per_tile = stack.enter_context(tc.tile_pool(name="per_tile", bufs=2 * SET))
+        psum = stack.enter_context(tc.psum_pool(name="psum", bufs=SET))
+
+        d_view = distance_matrix.rearrange("b i j k -> (b i) j k")
+        d_sets = []
+
+        def load_distances(s):
+            d_sb = d_pool.tile([P, SET, ND], BF16, name="d_sb")
+            nc.sync.dma_start(out=d_sb[:], in_=d_view[:, s * SET : (s + 1) * SET, :])
+            d_sets.append(d_sb)
+
+        w_planes = consts.tile([P, D_PASSES + 1, NH], U8, align_bytes=64)
+        nc.vector.memset(w_planes[:].bitcast(I32), 0)
+        wdf_words = consts.tile([P, D_PASSES, NH], U32, align_bytes=64)
+        wfc_words = consts.tile([P, NF], U32, align_bytes=64)
+
+        load_distances(0)
+        nc.sync.dma_start(
+            out=wdf_words[:].bitcast(I32),
+            in_=W_df_words.rearrange("g p n t -> p g (n t)").bitcast(I32),
+        )
+        for r in range(4):
+            nc.sync.dma_start(
+                out=w_planes[r:P:32, 0:D_PASSES, :].bitcast(I32),
+                in_=W_df_scales.bitcast(I32)[:, r:16:4, :].rearrange("g q n -> q g n"),
+            )
+        load_distances(1)
+        nc.sync.dma_start(
+            out=wfc_words[:].bitcast(I32),
+            in_=W_fc_words.rearrange("g p n t -> p (g n t)").bitcast(I32),
+        )
+        for r in range(4):
+            nc.sync.dma_start(
+                out=w_planes[r:P:32, D_PASSES, :].bitcast(I32),
+                in_=W_fc_scales.bitcast(I32)[0, r:16:4, :],
+            )
+        for s in range(2, SETS):
+            load_distances(s)
+
+        a_sb = consts.tile([P, NF], BF16)
+        nc.scalar.dma_start(out=a_sb[:], in_=atom_features.rearrange("b n f -> (b n) f"))
+        wcf_sb = consts.tile([P, F_CHUNKS, NH], BF16)
+        nc.scalar.dma_start(out=wcf_sb[:], in_=W_cf.rearrange("(c f) h -> f c h", f=P))
+        bcf_bf = consts.tile([P, PACK], BF16)
+        nc.scalar.dma_start(out=bcf_bf[:], in_=b_cf.rearrange("(p t) -> p t", t=PACK))
+        bdf_bf = consts.tile([P, NH], BF16)
+        nc.scalar.dma_start(out=bdf_bf[:], in_=b_df.partition_broadcast(P))
+        mask_bf = consts.tile([P, ATOMS], BF16)
+        nc.scalar.dma_start(out=mask_bf[:], in_=distance_matrix_mask.rearrange("b i j -> (b i) j"))
+
+        ident_f32 = consts.tile([P, P], F32)
+        make_identity(nc, ident_f32[:])
+        ident_bf = consts.tile([P, P], BF16)
+        make_identity(nc, ident_bf[:])
+
+        warm = consts.tile([P, 1], F32)
+        nc.vector.memset(warm[:], 0.0)
+        nc.scalar.activation(out=warm[:], in_=warm[:], func=TANH)
+
+        mask_f32 = consts.tile([P, ATOMS], F32)
+        bcf_f32 = consts.tile([P, PACK], F32)
+        bdf_sorted = consts.tile([P, PACK, P], F32)
+        sums = [consts.tile([P, NF], F32, name="sum_%d" % e) for e in range(SET)]
+
+        def widen_small_operands():
+            nc.vector.tensor_copy(out=bdf_sorted[:], in_=bdf_bf[:].rearrange("q (p t) -> q t p", t=PACK))
+            nc.vector.tensor_copy(out=bcf_f32[:], in_=bcf_bf[:])
+            nc.vector.tensor_copy(out=mask_f32[:], in_=mask_bf[:])
+            nc.vector.tensor_copy(out=sums[0][:], in_=a_sb[:])
+            nc.vector.memset(sums[1][:], 0.0)
+
+        atom_t = consts.tile([P, ATOMS, MOLS, PACK], F32)
+
+        def atom_layer():
+            at_ps = psum.tile([P, F_CHUNKS, P], BF16, tag="xt", name="at_ps")
+            for c in range(F_CHUNKS):
+                nc.tensor.transpose(out=at_ps[:, c, :], in_=a_sb[:, c * P : (c + 1) * P], identity=ident_bf[:])
+            a_t = consts.tile([P, F_CHUNKS, P], BF16)
+            nc.scalar.copy(out=a_t[:], in_=at_ps[:])
+            ah_ps = psum.tile([P, PACK, P], F32, tag="xt", name="ah_ps")
+            for t in range(PACK):
+                for c in range(F_CHUNKS):
+                    nc.tensor.matmul(
+                        out=ah_ps[:, t, :],
+                        lhsT=wcf_sb[:, c, t:NH:PACK],
+                        rhs=a_t[:, c, :],
+                        start=(c == 0),
+                        stop=(c == F_CHUNKS - 1),
+                    )
+            nc.vector.tensor_tensor(
+                out=atom_t[:],
+                in0=ah_ps[:].rearrange("p t (b j) -> p j b t", b=MOLS),
+                in1=bcf_f32[:].unsqueeze(1).unsqueeze(1).to_broadcast([P, ATOMS, MOLS, PACK]),
+                op=ADD,
+            )
+
+        d_grouped, d_codes, hidden, xt_banks, g_grouped, g_codes = {}, {}, {}, {}, {}, {}
+
+        def transpose_distances(s):
+            grouped = work.tile([P, SET, D_PASSES, P, PACK], BF16, align_bytes=64, name="d_grouped")
+            for r in range(SET):
+                d_words = d_sets[s][:, r, :].bitcast(F32)
+                dt_ps = psum.tile([P, D_PASSES, 2, P], F32, tag="dt", name="dt_ps")
+                for g in range(D_PASSES):
+                    for u in range(2):
+                        nc.tensor.transpose(
+                            out=dt_ps[:, g, u, :],
+                            in_=d_words[:, 256 * g + u : 256 * (g + 1) : 2],
+                            identity=ident_f32[:],
+                        )
+                nc.scalar.copy(out=grouped[:, r].bitcast(F32), in_=dt_ps[:].rearrange("p g u c -> p g c u"))
+            d_grouped[s] = grouped
+
+        def quantise_distances(s):
+            words = work.tile([P, SET, D_PASSES, P], U32, align_bytes=64, name="d_words")
+            plane = work.tile([P, SET, D_PASSES, P], U8, align_bytes=64, name="d_plane")
+            nc.vector.quantize_mx(
+                out=words[:].rearrange("p r g c -> p (r g c)").bitcast(FP8X4),
+                scales=plane[:].rearrange("p r g c -> p (r g c)"),
+                in_=d_grouped[s][:].rearrange("p r g c t -> p (r g c t)"),
+            )
+            d_codes[s] = (words, plane)
+
+        def first_matmul(s):
+            words, plane = d_codes[s]
+            hidden[s] = []
+            for r in range(SET):
+                s1_ps = psum.tile([P, NH], F32, tag="s1", name="s1_ps")
+                for g in range(D_PASSES):
+                    nc.tensor.matmul_mx(
+                        out=s1_ps[:],
+                        lhsT=words[:, r, g, :].bitcast(FP8X4),
+                        lhsT_scale=plane[:, r, g, :],
+                        rhs=wdf_words[:, g, :].bitcast(FP8X4),
+                        rhs_scale=w_planes[:, g, :],
+                        start=(g == 0),
+                        stop=(g == D_PASSES - 1),
+                    )
+                x_sb = per_tile.tile([P, PACK, P], F32, name="x_sb")
+                nc.vector.tensor_tensor(
+                    out=x_sb[:],
+                    in0=s1_ps[:].rearrange("q (p t) -> q t p", t=PACK),
+                    in1=bdf_sorted[:],
+                    op=ADD,
+                )
+                hidden[s].append(x_sb)
+
+        def transpose_hidden(s):
+            xt_banks[s] = []
+            for r in range(SET):
+                xt_ps = psum.tile([P, PACK, P], F32, tag="xt", name="xt_ps")
+                for t in range(PACK):
+                    nc.tensor.transpose(out=xt_ps[:, t, :], in_=hidden[s][r][:, t, :], identity=ident_f32[:])
+                xt_banks[s].append(xt_ps)
+
+        def gate(s):
+            grouped = work.tile([P, SET, P, PACK], BF16, align_bytes=64, name="g_grouped")
+            for r in range(SET):
+                j = s * SET + r
+                nc.vector.tensor_tensor(
+                    out=grouped[:, r].rearrange("p (b i) t -> p b i t", b=MOLS),
+                    in0=xt_banks[s][r][:].rearrange("p t (b i) -> p b i t", b=MOLS),
+                    in1=atom_t[:, j].unsqueeze(2).to_broadcast([P, MOLS, ATOMS, PACK]),
+                    op=MULT,
+                )
+            g_grouped[s] = grouped
+
+        def quantise_gated(s):
+            words = work.tile([P, SET, P], U32, align_bytes=64, name="g_words")
+            plane = work.tile([P, SET, P], U8, align_bytes=64, name="g_plane")
+            nc.vector.quantize_mx(
+                out=words[:].rearrange("p r c -> p (r c)").bitcast(FP8X4),
+                scales=plane[:].rearrange("p r c -> p (r c)"),
+                in_=g_grouped[s][:].rearrange("p r c t -> p (r c t)"),
+            )
+            g_codes[s] = (words, plane)
+
+        def second_matmul(s):
+            words, plane = g_codes[s]
+            for r in range(SET):
+                j = s * SET + r
+                s2_ps = psum.tile([P, NF], F32, tag="s2", name="s2_ps")
+                nc.tensor.matmul_mx(
+                    out=s2_ps[:],
+                    lhsT=words[:, r, :].bitcast(FP8X4),
+                    lhsT_scale=plane[:, r, :],
+                    rhs=wfc_words[:].bitcast(FP8X4),
+                    rhs_scale=w_planes[:, D_PASSES, :],
+                    start=True,
+                    stop=True,
+                )
+                th_sb = per_tile.tile([P, NF], F32, name="th_sb")
+                nc.scalar.activation(out=th_sb[:], in_=s2_ps[:], func=TANH, scale=mask_f32[:, j : j + 1])
+                nc.gpsimd.tensor_tensor(out=sums[r][:], in0=sums[r][:], in1=th_sb[:], op=ADD)
+
+        def live(s):
+            return 0 <= s < SETS
+
+        for step in range(SETS + 3):
+            if live(step):
+                transpose_distances(step)
+            if live(step - 2):
+                transpose_hidden(step - 2)
+                gate(step - 2)
+            if live(step):
+                quantise_distances(step)
+            if live(step - 2):
+                quantise_gated(step - 2)
+            if live(step - 1):
+                first_matmul(step - 1)
+            if live(step - 3):
+                second_matmul(step - 3)
+            if step == 0:
+                widen_small_operands()
+                atom_layer()
+
+        result = consts.tile([P, NF], F32)
+        nc.vector.tensor_tensor(out=result[:], in0=sums[0][:], in1=sums[1][:], op=ADD)
+        nc.sync.dma_start(out=out.rearrange("b i f -> (b i) f"), in_=result[:])

@@ -241,7 +241,7 @@ def tile_dtnnstep_pa_kernel(
                 )
                 th_sb = per_tile.tile([P, NF], F32, name="th_sb")
                 nc.scalar.activation(out=th_sb[:], in_=s2_ps[:], func=TANH, scale=mask_f32[:, j : j + 1])
-                nc.gpsimd.tensor_tensor(out=sums[r][:], in0=sums[r][:], in1=th_sb[:], op=ADD)
+                nc.vector.tensor_tensor(out=sums[r][:], in0=sums[r][:], in1=th_sb[:], op=ADD)
 
         def live(s):
             return 0 <= s < SETS

@@ -22,8 +22,11 @@ ND = 1024
 NH = 512
 D_PASSES = ND // (P * PACK)
 F_CHUNKS = NF // P
-SET = 2
-SETS = ATOMS // SET
+H_TILES = NH // P
+TILES = 4
+PAIRS = TILES * P
+CHUNKS = ATOMS // TILES
+QUAD = P // PACK
 
 FLOPS = 2 * MOLS * ATOMS * ATOMS * (ND * NH + NH * NF) + 2 * MOLS * ATOMS * NF * NH
 
@@ -46,18 +49,20 @@ def tile_dtnnstep_pa_kernel(
     with ExitStack() as stack:
         stack.enter_context(tc.manual_schedule())
         consts = stack.enter_context(tc.tile_pool(name="consts", bufs=1))
-        d_pool = stack.enter_context(tc.tile_pool(name="d_pool", bufs=SETS))
+        d_pool = stack.enter_context(tc.tile_pool(name="d_pool", bufs=CHUNKS))
         work = stack.enter_context(tc.tile_pool(name="work", bufs=2))
-        per_tile = stack.enter_context(tc.tile_pool(name="per_tile", bufs=2 * SET))
-        psum = stack.enter_context(tc.psum_pool(name="psum", bufs=SET))
+        th_pool = stack.enter_context(tc.tile_pool(name="th_pool", bufs=TILES))
+        psum = stack.enter_context(tc.psum_pool(name="psum", bufs=2))
 
         d_view = distance_matrix.rearrange("b i j k -> (b i) j k")
-        d_sets = []
+        d_chunks = {}
 
-        def load_distances(s):
-            d_sb = d_pool.tile([P, SET, ND], BF16, name="d_sb")
-            nc.sync.dma_start(out=d_sb[:], in_=d_view[:, s * SET : (s + 1) * SET, :])
-            d_sets.append(d_sb)
+        def load_distances(n):
+            d_sb = d_pool.tile([P, TILES, ND], BF16, name="d_sb")
+            for half in range(2):
+                r0 = 2 * half
+                nc.sync.dma_start(out=d_sb[:, r0 : r0 + 2, :], in_=d_view[:, n * TILES + r0 : n * TILES + r0 + 2, :])
+            d_chunks[n] = d_sb
 
         w_planes = consts.tile([P, D_PASSES + 1, NH], U8, align_bytes=64)
         nc.vector.memset(w_planes[:].bitcast(I32), 0)
@@ -84,17 +89,15 @@ def tile_dtnnstep_pa_kernel(
                 out=w_planes[r:P:32, D_PASSES, :].bitcast(I32),
                 in_=W_fc_scales.bitcast(I32)[0, r:16:4, :],
             )
-        for s in range(2, SETS):
-            load_distances(s)
 
         a_sb = consts.tile([P, NF], BF16)
         nc.scalar.dma_start(out=a_sb[:], in_=atom_features.rearrange("b n f -> (b n) f"))
         wcf_sb = consts.tile([P, F_CHUNKS, NH], BF16)
         nc.scalar.dma_start(out=wcf_sb[:], in_=W_cf.rearrange("(c f) h -> f c h", f=P))
-        bcf_bf = consts.tile([P, PACK], BF16)
-        nc.scalar.dma_start(out=bcf_bf[:], in_=b_cf.rearrange("(p t) -> p t", t=PACK))
-        bdf_bf = consts.tile([P, NH], BF16)
-        nc.scalar.dma_start(out=bdf_bf[:], in_=b_df.partition_broadcast(P))
+        bias_rows = consts.tile([P, P], BF16)
+        nc.vector.memset(bias_rows[:], 0.0)
+        nc.scalar.dma_start(out=bias_rows[0:H_TILES, :], in_=b_df.rearrange("(m x) -> m x", x=P))
+        nc.scalar.dma_start(out=bias_rows[H_TILES : 2 * H_TILES, :], in_=b_cf.rearrange("(m x) -> m x", x=P))
         mask_bf = consts.tile([P, ATOMS], BF16)
         nc.scalar.dma_start(out=mask_bf[:], in_=distance_matrix_mask.rearrange("b i j -> (b i) j"))
 
@@ -108,48 +111,45 @@ def tile_dtnnstep_pa_kernel(
         nc.scalar.activation(out=warm[:], in_=warm[:], func=TANH)
 
         mask_f32 = consts.tile([P, ATOMS], F32)
-        bcf_f32 = consts.tile([P, PACK], F32)
-        bdf_sorted = consts.tile([P, PACK, P], F32)
-        sums = [consts.tile([P, NF], F32, name="sum_%d" % e) for e in range(SET)]
+        sums = [consts.tile([P, NF], F32, name="sum_%d" % e) for e in range(2)]
+        bias_x = consts.tile([P, 2 * H_TILES], F32)
+        atom_x = consts.tile([P, H_TILES, ATOMS * MOLS], F32)
 
-        def widen_small_operands():
-            nc.vector.tensor_copy(out=bdf_sorted[:], in_=bdf_bf[:].rearrange("q (p t) -> q t p", t=PACK))
-            nc.vector.tensor_copy(out=bcf_f32[:], in_=bcf_bf[:])
+        def atom_layer():
             nc.vector.tensor_copy(out=mask_f32[:], in_=mask_bf[:])
             nc.vector.tensor_copy(out=sums[0][:], in_=a_sb[:])
             nc.vector.memset(sums[1][:], 0.0)
-
-        atom_t = consts.tile([P, ATOMS, MOLS, PACK], F32)
-
-        def atom_layer():
-            at_ps = psum.tile([P, F_CHUNKS, P], BF16, tag="xt", name="at_ps")
+            bias_ps = psum.tile([P, P], BF16, tag="s1", bufs=H_TILES, name="bias_ps")
+            nc.tensor.transpose(out=bias_ps[:], in_=bias_rows[:], identity=ident_bf[:])
+            nc.vector.tensor_copy(out=bias_x[:], in_=bias_ps[:, 0 : 2 * H_TILES])
+            at_ps = psum.tile([P, F_CHUNKS, P], BF16, tag="s1", bufs=H_TILES, name="at_ps")
             for c in range(F_CHUNKS):
                 nc.tensor.transpose(out=at_ps[:, c, :], in_=a_sb[:, c * P : (c + 1) * P], identity=ident_bf[:])
             a_t = consts.tile([P, F_CHUNKS, P], BF16)
             nc.scalar.copy(out=a_t[:], in_=at_ps[:])
-            ah_ps = psum.tile([P, PACK, P], F32, tag="xt", name="ah_ps")
-            for t in range(PACK):
+            ah_ps = psum.tile([P, H_TILES, P], F32, tag="s1", bufs=H_TILES, name="ah_ps")
+            for m in range(H_TILES):
                 for c in range(F_CHUNKS):
                     nc.tensor.matmul(
-                        out=ah_ps[:, t, :],
-                        lhsT=wcf_sb[:, c, t:NH:PACK],
+                        out=ah_ps[:, m, :],
+                        lhsT=wcf_sb[:, c, m * P : (m + 1) * P],
                         rhs=a_t[:, c, :],
                         start=(c == 0),
                         stop=(c == F_CHUNKS - 1),
                     )
             nc.vector.tensor_tensor(
-                out=atom_t[:],
-                in0=ah_ps[:].rearrange("p t (b j) -> p j b t", b=MOLS),
-                in1=bcf_f32[:].unsqueeze(1).unsqueeze(1).to_broadcast([P, ATOMS, MOLS, PACK]),
+                out=atom_x[:].rearrange("x m (j b) -> x m j b", b=MOLS),
+                in0=ah_ps[:].rearrange("x m (b j) -> x m j b", b=MOLS),
+                in1=bias_x[:, H_TILES : 2 * H_TILES].unsqueeze(2).unsqueeze(3).to_broadcast([P, H_TILES, ATOMS, MOLS]),
                 op=ADD,
             )
 
-        d_grouped, d_codes, hidden, xt_banks, g_grouped, g_codes = {}, {}, {}, {}, {}, {}
+        d_grouped, d_codes, moved, g_codes = {}, {}, {}, {}
 
-        def transpose_distances(s):
-            grouped = work.tile([P, SET, D_PASSES, P, PACK], BF16, align_bytes=64, name="d_grouped")
-            for r in range(SET):
-                d_words = d_sets[s][:, r, :].bitcast(F32)
+        def transpose_distances(n):
+            grouped = work.tile([P, D_PASSES, TILES, P, PACK], BF16, align_bytes=64, name="d_grouped")
+            for r in range(TILES):
+                d_words = d_chunks[n][:, r, :].bitcast(F32)
                 dt_ps = psum.tile([P, D_PASSES, 2, P], F32, tag="dt", name="dt_ps")
                 for g in range(D_PASSES):
                     for u in range(2):
@@ -158,111 +158,100 @@ def tile_dtnnstep_pa_kernel(
                             in_=d_words[:, 256 * g + u : 256 * (g + 1) : 2],
                             identity=ident_f32[:],
                         )
-                nc.scalar.copy(out=grouped[:, r].bitcast(F32), in_=dt_ps[:].rearrange("p g u c -> p g c u"))
-            d_grouped[s] = grouped
+                nc.scalar.copy(out=grouped[:, :, r].bitcast(F32), in_=dt_ps[:].rearrange("p g u c -> p g c u"))
+            d_grouped[n] = grouped
 
-        def quantise_distances(s):
-            words = work.tile([P, SET, D_PASSES, P], U32, align_bytes=64, name="d_words")
-            plane = work.tile([P, SET, D_PASSES, P], U8, align_bytes=64, name="d_plane")
+        def quantise_distances(n):
+            words = work.tile([P, D_PASSES, PAIRS], U32, align_bytes=64, name="d_words")
+            plane = work.tile([P, D_PASSES, PAIRS], U8, align_bytes=64, name="d_plane")
             nc.vector.quantize_mx(
-                out=words[:].rearrange("p r g c -> p (r g c)").bitcast(FP8X4),
-                scales=plane[:].rearrange("p r g c -> p (r g c)"),
-                in_=d_grouped[s][:].rearrange("p r g c t -> p (r g c t)"),
+                out=words[:].rearrange("p g c -> p (g c)").bitcast(FP8X4),
+                scales=plane[:].rearrange("p g c -> p (g c)"),
+                in_=d_grouped[n][:].rearrange("p g r c t -> p (g r c t)"),
             )
-            d_codes[s] = (words, plane)
+            d_codes[n] = (words, plane)
 
-        def first_matmul(s):
-            words, plane = d_codes[s]
-            hidden[s] = []
-            for r in range(SET):
-                s1_ps = psum.tile([P, NH], F32, tag="s1", name="s1_ps")
+        def first_matmul(n):
+            words, plane = d_codes[n]
+            gated = work.tile([P, H_TILES, PAIRS], BF16, name="gated")
+            by_word = work.tile([P, PACK, PAIRS], BF16, name="by_word")
+            for m in range(H_TILES):
+                s1_ps = psum.tile([P, PAIRS], F32, tag="s1", bufs=H_TILES, name="s1_ps")
                 for g in range(D_PASSES):
                     nc.tensor.matmul_mx(
                         out=s1_ps[:],
-                        lhsT=words[:, r, g, :].bitcast(FP8X4),
-                        lhsT_scale=plane[:, r, g, :],
-                        rhs=wdf_words[:, g, :].bitcast(FP8X4),
-                        rhs_scale=w_planes[:, g, :],
+                        lhsT=wdf_words[:, g, m * P : (m + 1) * P].bitcast(FP8X4),
+                        lhsT_scale=w_planes[:, g, m * P : (m + 1) * P],
+                        rhs=words[:, g, :].bitcast(FP8X4),
+                        rhs_scale=plane[:, g, :],
                         start=(g == 0),
                         stop=(g == D_PASSES - 1),
                     )
-                x_sb = per_tile.tile([P, PACK, P], F32, name="x_sb")
-                nc.vector.tensor_tensor(
-                    out=x_sb[:],
-                    in0=s1_ps[:].rearrange("q (p t) -> q t p", t=PACK),
-                    in1=bdf_sorted[:],
-                    op=ADD,
+                jb = TILES * MOLS
+                nc.vector.scalar_tensor_tensor(
+                    out=gated[:, m, :].rearrange("x (q i) -> x q i", i=ATOMS),
+                    in0=s1_ps[:].rearrange("x (q i) -> x q i", i=ATOMS),
+                    scalar=bias_x[:, m : m + 1],
+                    in1=atom_x[:, m, n * jb : (n + 1) * jb].unsqueeze(2).to_broadcast([P, jb, ATOMS]),
+                    op0=ADD,
+                    op1=MULT,
                 )
-                hidden[s].append(x_sb)
-
-        def transpose_hidden(s):
-            xt_banks[s] = []
-            for r in range(SET):
-                xt_ps = psum.tile([P, PACK, P], F32, tag="xt", name="xt_ps")
                 for t in range(PACK):
-                    nc.tensor.transpose(out=xt_ps[:, t, :], in_=hidden[s][r][:, t, :], identity=ident_f32[:])
-                xt_banks[s].append(xt_ps)
+                    nc.sync.dma_start(out=by_word[m * QUAD : (m + 1) * QUAD, t, :], in_=gated[t:P:PACK, m, :])
+            moved[n] = by_word
 
-        def gate(s):
-            grouped = work.tile([P, SET, P, PACK], BF16, align_bytes=64, name="g_grouped")
-            for r in range(SET):
-                j = s * SET + r
-                nc.vector.tensor_tensor(
-                    out=grouped[:, r].rearrange("p (b i) t -> p b i t", b=MOLS),
-                    in0=xt_banks[s][r][:].rearrange("p t (b i) -> p b i t", b=MOLS),
-                    in1=atom_t[:, j].unsqueeze(2).to_broadcast([P, MOLS, ATOMS, PACK]),
-                    op=MULT,
-                )
-            g_grouped[s] = grouped
-
-        def quantise_gated(s):
-            words = work.tile([P, SET, P], U32, align_bytes=64, name="g_words")
-            plane = work.tile([P, SET, P], U8, align_bytes=64, name="g_plane")
-            nc.vector.quantize_mx(
-                out=words[:].rearrange("p r c -> p (r c)").bitcast(FP8X4),
-                scales=plane[:].rearrange("p r c -> p (r c)"),
-                in_=g_grouped[s][:].rearrange("p r c t -> p (r c t)"),
+        def quantise_gated(n):
+            grouped = work.tile([P, PAIRS, PACK], BF16, align_bytes=64, name="g_grouped")
+            nc.scalar.copy(
+                out=grouped[:].rearrange("p (c i) t -> p c t i", i=4),
+                in_=moved[n][:].rearrange("p t (c i) -> p c t i", i=4),
             )
-            g_codes[s] = (words, plane)
+            words = work.tile([P, PAIRS], U32, align_bytes=64, name="g_words")
+            plane = work.tile([P, PAIRS], U8, align_bytes=64, name="g_plane")
+            nc.vector.quantize_mx(
+                out=words[:].bitcast(FP8X4),
+                scales=plane[:],
+                in_=grouped[:].rearrange("p c t -> p (c t)"),
+            )
+            g_codes[n] = (words, plane)
 
-        def second_matmul(s):
-            words, plane = g_codes[s]
-            for r in range(SET):
-                j = s * SET + r
+        def second_matmul(n, tiles):
+            words, plane = g_codes[n]
+            for r in tiles:
+                j = n * TILES + r
                 s2_ps = psum.tile([P, NF], F32, tag="s2", name="s2_ps")
                 nc.tensor.matmul_mx(
                     out=s2_ps[:],
-                    lhsT=words[:, r, :].bitcast(FP8X4),
-                    lhsT_scale=plane[:, r, :],
+                    lhsT=words[:, r * P : (r + 1) * P].bitcast(FP8X4),
+                    lhsT_scale=plane[:, r * P : (r + 1) * P],
                     rhs=wfc_words[:].bitcast(FP8X4),
                     rhs_scale=w_planes[:, D_PASSES, :],
                     start=True,
                     stop=True,
                 )
-                th_sb = per_tile.tile([P, NF], F32, name="th_sb")
+                th_sb = th_pool.tile([P, NF], F32, name="th_sb")
                 nc.scalar.activation(out=th_sb[:], in_=s2_ps[:], func=TANH, scale=mask_f32[:, j : j + 1])
-                nc.vector.tensor_tensor(out=sums[r][:], in0=sums[r][:], in1=th_sb[:], op=ADD)
+                nc.vector.tensor_tensor(out=sums[r % 2][:], in0=sums[r % 2][:], in1=th_sb[:], op=ADD)
 
-        def live(s):
-            return 0 <= s < SETS
+        def live(n):
+            return 0 <= n < CHUNKS
 
-        for step in range(SETS + 3):
+        for step in range(CHUNKS + 3):
+            if live(step + 2):
+                load_distances(step + 2)
             if live(step):
                 transpose_distances(step)
-            if live(step - 2):
-                transpose_hidden(step - 2)
-                gate(step - 2)
-            if live(step):
                 quantise_distances(step)
-            if live(step - 2):
-                quantise_gated(step - 2)
+            if step == 0:
+                atom_layer()
+            if live(step - 3):
+                second_matmul(step - 3, (0, 1))
             if live(step - 1):
                 first_matmul(step - 1)
+            if live(step - 2):
+                quantise_gated(step - 2)
             if live(step - 3):
-                second_matmul(step - 3)
-            if step == 0:
-                widen_small_operands()
-                atom_layer()
+                second_matmul(step - 3, (2, 3))
 
         result = consts.tile([P, NF], F32)
         nc.vector.tensor_tensor(out=result[:], in0=sums[0][:], in1=sums[1][:], op=ADD)

@@ -50,8 +50,8 @@ def tile_dtnnstep_pa_kernel(
         stack.enter_context(tc.manual_schedule())
         consts = stack.enter_context(tc.tile_pool(name="consts", bufs=1))
         d_pool = stack.enter_context(tc.tile_pool(name="d_pool", bufs=CHUNKS))
-        work = stack.enter_context(tc.tile_pool(name="work", bufs=2))
-        th_pool = stack.enter_context(tc.tile_pool(name="th_pool", bufs=TILES))
+        work = stack.enter_context(tc.tile_pool(name="work", bufs=3))
+        th_pool = stack.enter_context(tc.tile_pool(name="th_pool", bufs=2 * TILES))
         psum = stack.enter_context(tc.psum_pool(name="psum", bufs=2))
 
         d_view = distance_matrix.rearrange("b i j k -> (b i) j k")
@@ -236,7 +236,7 @@ def tile_dtnnstep_pa_kernel(
         def live(n):
             return 0 <= n < CHUNKS
 
-        for step in range(CHUNKS + 3):
+        for step in range(CHUNKS + 4):
             if live(step + 2):
                 load_distances(step + 2)
             if live(step):
@@ -244,14 +244,12 @@ def tile_dtnnstep_pa_kernel(
                 quantise_distances(step)
             if step == 0:
                 atom_layer()
-            if live(step - 3):
-                second_matmul(step - 3, (0, 1))
             if live(step - 1):
                 first_matmul(step - 1)
-            if live(step - 2):
-                quantise_gated(step - 2)
             if live(step - 3):
-                second_matmul(step - 3, (2, 3))
+                quantise_gated(step - 3)
+            if live(step - 4):
+                second_matmul(step - 4, (0, 1, 2, 3))
 
         result = consts.tile([P, NF], F32)
         nc.vector.tensor_tensor(out=result[:], in0=sums[0][:], in1=sums[1][:], op=ADD)

@@ -27,6 +27,7 @@ TILES = 4
 PAIRS = TILES * P
 CHUNKS = ATOMS // TILES
 QUAD = P // PACK
+HALF = 2
 
 FLOPS = 2 * MOLS * ATOMS * ATOMS * (ND * NH + NH * NF) + 2 * MOLS * ATOMS * NF * NH
 
@@ -51,7 +52,7 @@ def tile_dtnnstep_pa_kernel(
         consts = stack.enter_context(tc.tile_pool(name="consts", bufs=1))
         d_pool = stack.enter_context(tc.tile_pool(name="d_pool", bufs=CHUNKS))
         work = stack.enter_context(tc.tile_pool(name="work", bufs=3))
-        th_pool = stack.enter_context(tc.tile_pool(name="th_pool", bufs=2 * TILES))
+        th_pool = stack.enter_context(tc.tile_pool(name="th_pool", bufs=3))
         psum = stack.enter_context(tc.psum_pool(name="psum", bufs=2))
 
         d_view = distance_matrix.rearrange("b i j k -> (b i) j k")
@@ -111,14 +112,14 @@ def tile_dtnnstep_pa_kernel(
         nc.scalar.activation(out=warm[:], in_=warm[:], func=TANH)
 
         mask_f32 = consts.tile([P, ATOMS], F32)
-        sums = [consts.tile([P, NF], F32, name="sum_%d" % e) for e in range(2)]
+        sums = consts.tile([P, HALF, NF], F32)
         bias_x = consts.tile([P, 2 * H_TILES], F32)
         atom_x = consts.tile([P, H_TILES, ATOMS * MOLS], F32)
 
         def atom_layer():
             nc.vector.tensor_copy(out=mask_f32[:], in_=mask_bf[:])
-            nc.vector.tensor_copy(out=sums[0][:], in_=a_sb[:])
-            nc.vector.memset(sums[1][:], 0.0)
+            nc.vector.tensor_copy(out=sums[:, 0, :], in_=a_sb[:])
+            nc.vector.memset(sums[:, 1, :], 0.0)
             bias_ps = psum.tile([P, P], BF16, tag="s1", bufs=H_TILES, name="bias_ps")
             nc.tensor.transpose(out=bias_ps[:], in_=bias_rows[:], identity=ident_bf[:])
             nc.vector.tensor_copy(out=bias_x[:], in_=bias_ps[:, 0 : 2 * H_TILES])
@@ -144,11 +145,16 @@ def tile_dtnnstep_pa_kernel(
                 op=ADD,
             )
 
-        d_grouped, d_codes, moved, g_codes = {}, {}, {}, {}
+        d_grouped, d_codes, gated_tiles, moved, g_codes = {}, {}, {}, {}, {}
 
-        def transpose_distances(n):
-            grouped = work.tile([P, D_PASSES, TILES, P, PACK], BF16, align_bytes=64, name="d_grouped")
-            for r in range(TILES):
+        def run(h):
+            return range(h * HALF, (h + 1) * HALF)
+
+        def transpose_distances(n, h):
+            if h == 0:
+                d_grouped[n] = work.tile([P, D_PASSES, TILES, P, PACK], BF16, align_bytes=64, name="d_grouped")
+            grouped = d_grouped[n]
+            for r in run(h):
                 d_words = d_chunks[n][:, r, :].bitcast(F32)
                 dt_ps = psum.tile([P, D_PASSES, 2, P], F32, tag="dt", name="dt_ps")
                 for g in range(D_PASSES):
@@ -159,7 +165,6 @@ def tile_dtnnstep_pa_kernel(
                             identity=ident_f32[:],
                         )
                 nc.scalar.copy(out=grouped[:, :, r].bitcast(F32), in_=dt_ps[:].rearrange("p g u c -> p g c u"))
-            d_grouped[n] = grouped
 
         def quantise_distances(n):
             words = work.tile([P, D_PASSES, PAIRS], U32, align_bytes=64, name="d_words")
@@ -171,11 +176,13 @@ def tile_dtnnstep_pa_kernel(
             )
             d_codes[n] = (words, plane)
 
-        def first_matmul(n):
+        def first_matmul(n, h):
             words, plane = d_codes[n]
-            gated = work.tile([P, H_TILES, PAIRS], BF16, name="gated")
-            by_word = work.tile([P, PACK, PAIRS], BF16, name="by_word")
-            for m in range(H_TILES):
+            if h == 0:
+                gated_tiles[n] = work.tile([P, H_TILES, PAIRS], BF16, name="gated")
+                moved[n] = work.tile([P, PACK, PAIRS], BF16, name="by_word")
+            gated, by_word = gated_tiles[n], moved[n]
+            for m in run(h):
                 s1_ps = psum.tile([P, PAIRS], F32, tag="s1", bufs=H_TILES, name="s1_ps")
                 for g in range(D_PASSES):
                     nc.tensor.matmul_mx(
@@ -198,7 +205,6 @@ def tile_dtnnstep_pa_kernel(
                 )
                 for t in range(PACK):
                     nc.sync.dma_start(out=by_word[m * QUAD : (m + 1) * QUAD, t, :], in_=gated[t:P:PACK, m, :])
-            moved[n] = by_word
 
         def quantise_gated(n):
             grouped = work.tile([P, PAIRS, PACK], BF16, align_bytes=64, name="g_grouped")
@@ -215,9 +221,10 @@ def tile_dtnnstep_pa_kernel(
             )
             g_codes[n] = (words, plane)
 
-        def second_matmul(n, tiles):
+        def second_matmul(n, h):
             words, plane = g_codes[n]
-            for r in tiles:
+            th_sb = th_pool.tile([P, HALF, NF], F32, name="th_sb")
+            for r in run(h):
                 j = n * TILES + r
                 s2_ps = psum.tile([P, NF], F32, tag="s2", name="s2_ps")
                 nc.tensor.matmul_mx(
@@ -229,9 +236,8 @@ def tile_dtnnstep_pa_kernel(
                     start=True,
                     stop=True,
                 )
-                th_sb = th_pool.tile([P, NF], F32, name="th_sb")
-                nc.scalar.activation(out=th_sb[:], in_=s2_ps[:], func=TANH, scale=mask_f32[:, j : j + 1])
-                nc.vector.tensor_tensor(out=sums[r % 2][:], in0=sums[r % 2][:], in1=th_sb[:], op=ADD)
+                nc.scalar.activation(out=th_sb[:, r % HALF, :], in_=s2_ps[:], func=TANH, scale=mask_f32[:, j : j + 1])
+            nc.vector.tensor_tensor(out=sums[:], in0=sums[:], in1=th_sb[:], op=ADD)
 
         def live(n):
             return 0 <= n < CHUNKS
@@ -239,18 +245,21 @@ def tile_dtnnstep_pa_kernel(
         for step in range(CHUNKS + 4):
             if live(step + 2):
                 load_distances(step + 2)
-            if live(step):
-                transpose_distances(step)
-                quantise_distances(step)
-            if step == 0:
-                atom_layer()
-            if live(step - 1):
-                first_matmul(step - 1)
-            if live(step - 3):
-                quantise_gated(step - 3)
-            if live(step - 4):
-                second_matmul(step - 4, (0, 1, 2, 3))
+            for h in range(TILES // HALF):
+                last = h == TILES // HALF - 1
+                if live(step):
+                    transpose_distances(step, h)
+                if last and live(step):
+                    quantise_distances(step)
+                if last and step == 0:
+                    atom_layer()
+                if live(step - 1):
+                    first_matmul(step - 1, h)
+                if last and live(step - 3):
+                    quantise_gated(step - 3)
+                if live(step - 4):
+                    second_matmul(step - 4, h)
 
         result = consts.tile([P, NF], F32)
-        nc.vector.tensor_tensor(out=result[:], in0=sums[0][:], in1=sums[1][:], op=ADD)
+        nc.vector.tensor_tensor(out=result[:], in0=sums[:, 0, :], in1=sums[:, 1, :], op=ADD)
         nc.sync.dma_start(out=out.rearrange("b i f -> (b i) f"), in_=result[:])

@@ -242,7 +242,7 @@ def tile_dtnnstep_pa_kernel(
         def live(n):
             return 0 <= n < CHUNKS
 
-        for step in range(CHUNKS + 4):
+        for step in range(CHUNKS + 3):
             if live(step + 2):
                 load_distances(step + 2)
             for h in range(TILES // HALF):
@@ -255,10 +255,10 @@ def tile_dtnnstep_pa_kernel(
                     atom_layer()
                 if live(step - 1):
                     first_matmul(step - 1, h)
-                if last and live(step - 3):
-                    quantise_gated(step - 3)
-                if live(step - 4):
-                    second_matmul(step - 4, h)
+                if last and live(step - 2):
+                    quantise_gated(step - 2)
+                if live(step - 3):
+                    second_matmul(step - 3, h)
 
         result = consts.tile([P, NF], F32)
         nc.vector.tensor_tensor(out=result[:], in0=sums[:, 0, :], in1=sums[:, 1, :], op=ADD)

@@ -26,7 +26,9 @@ H_TILES = NH // P
 TILES = 4
 PAIRS = TILES * P
 CHUNKS = ATOMS // TILES
-QUAD = P // PACK
+LAG_FIRST = 2
+LAG_GROUP = 4
+LAG_SECOND = 5
 HALF = 2
 
 FLOPS = 2 * MOLS * ATOMS * ATOMS * (ND * NH + NH * NF) + 2 * MOLS * ATOMS * NF * NH
@@ -67,12 +69,14 @@ def tile_dtnnstep_pa_kernel(
 
         w_planes = consts.tile([P, D_PASSES + 1, NH], U8, align_bytes=64)
         nc.vector.memset(w_planes[:].bitcast(I32), 0)
+        wdf_raw = consts.tile([P, D_PASSES, NH], U32, align_bytes=64)
         wdf_words = consts.tile([P, D_PASSES, NH], U32, align_bytes=64)
+        wdf_planes = consts.tile([P, D_PASSES, NH], U8, align_bytes=64)
         wfc_words = consts.tile([P, NF], U32, align_bytes=64)
 
         load_distances(0)
         nc.sync.dma_start(
-            out=wdf_words[:].bitcast(I32),
+            out=wdf_raw[:].bitcast(I32),
             in_=W_df_words.rearrange("g p n t -> p g (n t)").bitcast(I32),
         )
         for r in range(4):
@@ -95,10 +99,10 @@ def tile_dtnnstep_pa_kernel(
         nc.scalar.dma_start(out=a_sb[:], in_=atom_features.rearrange("b n f -> (b n) f"))
         wcf_sb = consts.tile([P, F_CHUNKS, NH], BF16)
         nc.scalar.dma_start(out=wcf_sb[:], in_=W_cf.rearrange("(c f) h -> f c h", f=P))
-        bias_rows = consts.tile([P, P], BF16)
-        nc.vector.memset(bias_rows[:], 0.0)
-        nc.scalar.dma_start(out=bias_rows[0:H_TILES, :], in_=b_df.rearrange("(m x) -> m x", x=P))
-        nc.scalar.dma_start(out=bias_rows[H_TILES : 2 * H_TILES, :], in_=b_cf.rearrange("(m x) -> m x", x=P))
+        bdf_bf = consts.tile([P, PACK], BF16)
+        nc.scalar.dma_start(out=bdf_bf[:], in_=b_df.rearrange("(p t) -> p t", t=PACK))
+        bcf_bf = consts.tile([P, PACK], BF16)
+        nc.scalar.dma_start(out=bcf_bf[:], in_=b_cf.rearrange("(p t) -> p t", t=PACK))
         mask_bf = consts.tile([P, ATOMS], BF16)
         nc.scalar.dma_start(out=mask_bf[:], in_=distance_matrix_mask.rearrange("b i j -> (b i) j"))
 
@@ -111,6 +115,15 @@ def tile_dtnnstep_pa_kernel(
         nc.vector.memset(warm[:], 0.0)
         nc.scalar.activation(out=warm[:], in_=warm[:], func=TANH)
 
+        nc.vector.tensor_copy(
+            out=wdf_words[:].bitcast(I32).rearrange("p g (t y) -> p g t y", t=PACK),
+            in_=wdf_raw[:].bitcast(I32).rearrange("p g (y t) -> p g t y", t=PACK),
+        )
+        nc.vector.tensor_copy(
+            out=wdf_planes[:].rearrange("p g (t y) -> p g t y", t=PACK),
+            in_=w_planes[:, 0:D_PASSES, :].rearrange("p g (y t) -> p g t y", t=PACK),
+        )
+
         mask_f32 = consts.tile([P, ATOMS], F32)
         sums = consts.tile([P, HALF, NF], F32)
         bias_x = consts.tile([P, 2 * H_TILES], F32)
@@ -120,9 +133,8 @@ def tile_dtnnstep_pa_kernel(
             nc.vector.tensor_copy(out=mask_f32[:], in_=mask_bf[:])
             nc.vector.tensor_copy(out=sums[:, 0, :], in_=a_sb[:])
             nc.vector.memset(sums[:, 1, :], 0.0)
-            bias_ps = psum.tile([P, P], BF16, tag="s1", bufs=H_TILES, name="bias_ps")
-            nc.tensor.transpose(out=bias_ps[:], in_=bias_rows[:], identity=ident_bf[:])
-            nc.vector.tensor_copy(out=bias_x[:], in_=bias_ps[:, 0 : 2 * H_TILES])
+            nc.vector.tensor_copy(out=bias_x[:, 0:H_TILES], in_=bdf_bf[:])
+            nc.vector.tensor_copy(out=bias_x[:, H_TILES : 2 * H_TILES], in_=bcf_bf[:])
             at_ps = psum.tile([P, F_CHUNKS, P], BF16, tag="s1", bufs=H_TILES, name="at_ps")
             for c in range(F_CHUNKS):
                 nc.tensor.transpose(out=at_ps[:, c, :], in_=a_sb[:, c * P : (c + 1) * P], identity=ident_bf[:])
@@ -133,7 +145,7 @@ def tile_dtnnstep_pa_kernel(
                 for c in range(F_CHUNKS):
                     nc.tensor.matmul(
                         out=ah_ps[:, m, :],
-                        lhsT=wcf_sb[:, c, m * P : (m + 1) * P],
+                        lhsT=wcf_sb[:, c, m:NH:PACK],
                         rhs=a_t[:, c, :],
                         start=(c == 0),
                         stop=(c == F_CHUNKS - 1),
@@ -145,7 +157,7 @@ def tile_dtnnstep_pa_kernel(
                 op=ADD,
             )
 
-        d_grouped, d_codes, gated_tiles, moved, g_codes = {}, {}, {}, {}, {}
+        d_grouped, d_codes, gated_tiles, g_codes = {}, {}, {}, {}
 
         def run(h):
             return range(h * HALF, (h + 1) * HALF)
@@ -180,15 +192,14 @@ def tile_dtnnstep_pa_kernel(
             words, plane = d_codes[n]
             if h == 0:
                 gated_tiles[n] = work.tile([P, H_TILES, PAIRS], BF16, name="gated")
-                moved[n] = work.tile([P, PACK, PAIRS], BF16, name="by_word")
-            gated, by_word = gated_tiles[n], moved[n]
+            gated = gated_tiles[n]
             for m in run(h):
                 s1_ps = psum.tile([P, PAIRS], F32, tag="s1", bufs=H_TILES, name="s1_ps")
                 for g in range(D_PASSES):
                     nc.tensor.matmul_mx(
                         out=s1_ps[:],
                         lhsT=wdf_words[:, g, m * P : (m + 1) * P].bitcast(FP8X4),
-                        lhsT_scale=w_planes[:, g, m * P : (m + 1) * P],
+                        lhsT_scale=wdf_planes[:, g, m * P : (m + 1) * P],
                         rhs=words[:, g, :].bitcast(FP8X4),
                         rhs_scale=plane[:, g, :],
                         start=(g == 0),
@@ -203,34 +214,33 @@ def tile_dtnnstep_pa_kernel(
                     op0=ADD,
                     op1=MULT,
                 )
-                for t in range(PACK):
-                    nc.sync.dma_start(out=by_word[m * QUAD : (m + 1) * QUAD, t, :], in_=gated[t:P:PACK, m, :])
 
-        def quantise_gated(n):
-            grouped = work.tile([P, PAIRS, PACK], BF16, align_bytes=64, name="g_grouped")
+        def quantise_gated(n, h):
+            cols = HALF * P
+            grouped = work.tile([P, cols, PACK], BF16, align_bytes=64, name="g_grouped")
             nc.scalar.copy(
                 out=grouped[:].rearrange("p (c i) t -> p c t i", i=4),
-                in_=moved[n][:].rearrange("p t (c i) -> p c t i", i=4),
+                in_=gated_tiles[n][:, :, h * cols : (h + 1) * cols].rearrange("p t (c i) -> p c t i", i=4),
             )
-            words = work.tile([P, PAIRS], U32, align_bytes=64, name="g_words")
-            plane = work.tile([P, PAIRS], U8, align_bytes=64, name="g_plane")
+            words = work.tile([P, cols], U32, align_bytes=64, name="g_words")
+            plane = work.tile([P, cols], U8, align_bytes=64, name="g_plane")
             nc.vector.quantize_mx(
                 out=words[:].bitcast(FP8X4),
                 scales=plane[:],
                 in_=grouped[:].rearrange("p c t -> p (c t)"),
             )
-            g_codes[n] = (words, plane)
+            g_codes[n, h] = (words, plane)
 
         def second_matmul(n, h):
-            words, plane = g_codes[n]
+            words, plane = g_codes[n, h]
             th_sb = th_pool.tile([P, HALF, NF], F32, name="th_sb")
             for r in run(h):
                 j = n * TILES + r
                 s2_ps = psum.tile([P, NF], F32, tag="s2", name="s2_ps")
                 nc.tensor.matmul_mx(
                     out=s2_ps[:],
-                    lhsT=words[:, r * P : (r + 1) * P].bitcast(FP8X4),
-                    lhsT_scale=plane[:, r * P : (r + 1) * P],
+                    lhsT=words[:, (r % HALF) * P : (r % HALF + 1) * P].bitcast(FP8X4),
+                    lhsT_scale=plane[:, (r % HALF) * P : (r % HALF + 1) * P],
                     rhs=wfc_words[:].bitcast(FP8X4),
                     rhs_scale=w_planes[:, D_PASSES, :],
                     start=True,
@@ -239,26 +249,26 @@ def tile_dtnnstep_pa_kernel(
                 nc.scalar.activation(out=th_sb[:, r % HALF, :], in_=s2_ps[:], func=TANH, scale=mask_f32[:, j : j + 1])
             nc.vector.tensor_tensor(out=sums[:], in0=sums[:], in1=th_sb[:], op=ADD)
 
-        def live(n):
-            return 0 <= n < CHUNKS
+        halves = CHUNKS * (TILES // HALF)
 
-        for step in range(CHUNKS + 3):
-            if live(step + 2):
-                load_distances(step + 2)
-            for h in range(TILES // HALF):
-                last = h == TILES // HALF - 1
-                if live(step):
-                    transpose_distances(step, h)
-                if last and live(step):
-                    quantise_distances(step)
-                if last and step == 0:
-                    atom_layer()
-                if live(step - 1):
-                    first_matmul(step - 1, h)
-                if last and live(step - 2):
-                    quantise_gated(step - 2)
-                if live(step - 3):
-                    second_matmul(step - 3, h)
+        def live(x):
+            return 0 <= x < halves
+
+        for k in range(halves + LAG_SECOND):
+            if k % 2 == 0 and live(k + 4):
+                load_distances(k // 2 + 2)
+            if live(k):
+                transpose_distances(k // 2, k % 2)
+                if k % 2 == 1:
+                    quantise_distances(k // 2)
+            if k == 1:
+                atom_layer()
+            if live(k - LAG_FIRST):
+                first_matmul((k - LAG_FIRST) // 2, (k - LAG_FIRST) % 2)
+            if live(k - LAG_GROUP):
+                quantise_gated((k - LAG_GROUP) // 2, (k - LAG_GROUP) % 2)
+            if live(k - LAG_SECOND):
+                second_matmul((k - LAG_SECOND) // 2, (k - LAG_SECOND) % 2)
 
         result = consts.tile([P, NF], F32)
         nc.vector.tensor_tensor(out=result[:], in0=sums[:, 0, :], in1=sums[:, 1, :], op=ADD)

@@ -22,14 +22,20 @@ ND = 1024
 NH = 512
 D_PASSES = ND // (P * PACK)
 F_CHUNKS = NF // P
-H_TILES = NH // P
-TILES = 4
+TILES = 2
 PAIRS = TILES * P
-CHUNKS = ATOMS // TILES
-LAG_FIRST = 2
-LAG_GROUP = 4
-LAG_SECOND = 5
-HALF = 2
+UNITS = ATOMS // TILES
+WORK_BUFS = 4
+DT_BUFS = 2
+S2_BUFS = 2
+S1_BUFS = 4
+TAIL_UNITS = 2
+LAG_QD = 0
+LAG_FIRST = 1
+LAG_GROUP = 2
+LAG_QG = 2
+LAG_SECOND = 3
+LAG_ADD = 3
 
 FLOPS = 2 * MOLS * ATOMS * ATOMS * (ND * NH + NH * NF) + 2 * MOLS * ATOMS * NF * NH
 
@@ -52,20 +58,17 @@ def tile_dtnnstep_pa_kernel(
     with ExitStack() as stack:
         stack.enter_context(tc.manual_schedule())
         consts = stack.enter_context(tc.tile_pool(name="consts", bufs=1))
-        d_pool = stack.enter_context(tc.tile_pool(name="d_pool", bufs=CHUNKS))
-        work = stack.enter_context(tc.tile_pool(name="work", bufs=3))
-        th_pool = stack.enter_context(tc.tile_pool(name="th_pool", bufs=3))
+        d_pool = stack.enter_context(tc.tile_pool(name="d_pool", bufs=UNITS))
+        work = stack.enter_context(tc.tile_pool(name="work", bufs=WORK_BUFS))
         psum = stack.enter_context(tc.psum_pool(name="psum", bufs=2))
 
         d_view = distance_matrix.rearrange("b i j k -> (b i) j k")
-        d_chunks = {}
+        d_units = {}
 
-        def load_distances(n):
+        def load_distances(u):
             d_sb = d_pool.tile([P, TILES, ND], BF16, name="d_sb")
-            for half in range(2):
-                r0 = 2 * half
-                nc.sync.dma_start(out=d_sb[:, r0 : r0 + 2, :], in_=d_view[:, n * TILES + r0 : n * TILES + r0 + 2, :])
-            d_chunks[n] = d_sb
+            nc.sync.dma_start(out=d_sb[:], in_=d_view[:, u * TILES : (u + 1) * TILES, :])
+            d_units[u] = d_sb
 
         w_planes = consts.tile([P, D_PASSES + 1, NH], U8, align_bytes=64)
         nc.vector.memset(w_planes[:].bitcast(I32), 0)
@@ -74,26 +77,39 @@ def tile_dtnnstep_pa_kernel(
         wdf_planes = consts.tile([P, D_PASSES, NH], U8, align_bytes=64)
         wfc_words = consts.tile([P, NF], U32, align_bytes=64)
 
+        def load_wdf_scales():
+            for r in range(4):
+                nc.sync.dma_start(
+                    out=w_planes[r:P:32, 0:D_PASSES, :].bitcast(I32),
+                    in_=W_df_scales.bitcast(I32)[:, r:16:4, :].rearrange("g q n -> q g n"),
+                )
+
+        def load_wdf_words():
+            nc.sync.dma_start(
+                out=wdf_raw[:].bitcast(I32),
+                in_=W_df_words.rearrange("g p n t -> p g (n t)").bitcast(I32),
+            )
+
+        def load_wfc():
+            nc.sync.dma_start(
+                out=wfc_words[:].bitcast(I32),
+                in_=W_fc_words.rearrange("g p n t -> p (g n t)").bitcast(I32),
+            )
+            for r in range(4):
+                nc.sync.dma_start(
+                    out=w_planes[r:P:32, D_PASSES, :].bitcast(I32),
+                    in_=W_fc_scales.bitcast(I32)[0, r:16:4, :],
+                )
+
         load_distances(0)
-        nc.sync.dma_start(
-            out=wdf_raw[:].bitcast(I32),
-            in_=W_df_words.rearrange("g p n t -> p g (n t)").bitcast(I32),
-        )
-        for r in range(4):
-            nc.sync.dma_start(
-                out=w_planes[r:P:32, 0:D_PASSES, :].bitcast(I32),
-                in_=W_df_scales.bitcast(I32)[:, r:16:4, :].rearrange("g q n -> q g n"),
-            )
+        load_wdf_words()
+        load_wdf_scales()
         load_distances(1)
-        nc.sync.dma_start(
-            out=wfc_words[:].bitcast(I32),
-            in_=W_fc_words.rearrange("g p n t -> p (g n t)").bitcast(I32),
-        )
-        for r in range(4):
-            nc.sync.dma_start(
-                out=w_planes[r:P:32, D_PASSES, :].bitcast(I32),
-                in_=W_fc_scales.bitcast(I32)[0, r:16:4, :],
-            )
+        load_distances(2)
+        load_distances(3)
+        load_wfc()
+        for u in range(4, UNITS):
+            load_distances(u)
 
         a_sb = consts.tile([P, NF], BF16)
         nc.scalar.dma_start(out=a_sb[:], in_=atom_features.rearrange("b n f -> (b n) f"))
@@ -106,170 +122,190 @@ def tile_dtnnstep_pa_kernel(
         mask_bf = consts.tile([P, ATOMS], BF16)
         nc.scalar.dma_start(out=mask_bf[:], in_=distance_matrix_mask.rearrange("b i j -> (b i) j"))
 
-        ident_f32 = consts.tile([P, P], F32)
-        make_identity(nc, ident_f32[:])
         ident_bf = consts.tile([P, P], BF16)
         make_identity(nc, ident_bf[:])
+        ident_f32 = consts.tile([P, P], F32)
+        make_identity(nc, ident_f32[:])
 
         warm = consts.tile([P, 1], F32)
         nc.vector.memset(warm[:], 0.0)
         nc.scalar.activation(out=warm[:], in_=warm[:], func=TANH)
 
-        nc.vector.tensor_copy(
-            out=wdf_words[:].bitcast(I32).rearrange("p g (t y) -> p g t y", t=PACK),
-            in_=wdf_raw[:].bitcast(I32).rearrange("p g (y t) -> p g t y", t=PACK),
-        )
-        nc.vector.tensor_copy(
-            out=wdf_planes[:].rearrange("p g (t y) -> p g t y", t=PACK),
-            in_=w_planes[:, 0:D_PASSES, :].rearrange("p g (y t) -> p g t y", t=PACK),
-        )
-
         mask_f32 = consts.tile([P, ATOMS], F32)
-        sums = consts.tile([P, HALF, NF], F32)
-        bias_x = consts.tile([P, 2 * H_TILES], F32)
-        atom_x = consts.tile([P, H_TILES, ATOMS * MOLS], F32)
+        sums = consts.tile([P, TILES, NF], F32)
+        bdf_x = consts.tile([P, PACK], F32)
+        bcf_x = consts.tile([P, PACK], F32)
+        atom_x = consts.tile([P, PACK, ATOMS * MOLS], F32)
+        a_t = consts.tile([P, F_CHUNKS, P], BF16)
 
-        def atom_layer():
-            nc.vector.tensor_copy(out=mask_f32[:], in_=mask_bf[:])
-            nc.vector.tensor_copy(out=sums[:, 0, :], in_=a_sb[:])
+        def reorder_scales():
+            nc.vector.tensor_copy(
+                out=wdf_planes[:].rearrange("p g (t y) -> p g t y", t=PACK),
+                in_=w_planes[:, 0:D_PASSES, :].rearrange("p g (y t) -> p g t y", t=PACK),
+            )
+
+        def reorder_words():
+            nc.vector.tensor_copy(
+                out=wdf_words[:].bitcast(I32).rearrange("p g (t y) -> p g t y", t=PACK),
+                in_=wdf_raw[:].bitcast(I32).rearrange("p g (y t) -> p g t y", t=PACK),
+            )
+
+        def small_casts():
             nc.vector.memset(sums[:, 1, :], 0.0)
-            nc.vector.tensor_copy(out=bias_x[:, 0:H_TILES], in_=bdf_bf[:])
-            nc.vector.tensor_copy(out=bias_x[:, H_TILES : 2 * H_TILES], in_=bcf_bf[:])
-            at_ps = psum.tile([P, F_CHUNKS, P], BF16, tag="s1", bufs=H_TILES, name="at_ps")
+            nc.vector.tensor_copy(out=sums[:, 0, :], in_=a_sb[:])
+            nc.vector.tensor_copy(out=bdf_x[:], in_=bdf_bf[:])
+            nc.vector.tensor_copy(out=bcf_x[:], in_=bcf_bf[:])
+            nc.vector.tensor_copy(out=mask_f32[:], in_=mask_bf[:])
+
+        def transpose_atoms():
+            at_ps = psum.tile([P, F_CHUNKS, P], BF16, tag="s1", bufs=S1_BUFS, name="at_ps")
             for c in range(F_CHUNKS):
                 nc.tensor.transpose(out=at_ps[:, c, :], in_=a_sb[:, c * P : (c + 1) * P], identity=ident_bf[:])
-            a_t = consts.tile([P, F_CHUNKS, P], BF16)
             nc.scalar.copy(out=a_t[:], in_=at_ps[:])
-            ah_ps = psum.tile([P, H_TILES, P], F32, tag="s1", bufs=H_TILES, name="ah_ps")
-            for m in range(H_TILES):
+
+        def atom_layer():
+            ah_ps = psum.tile([P, PACK, P], F32, tag="s1", bufs=S1_BUFS, name="ah_ps")
+            for t in range(PACK):
                 for c in range(F_CHUNKS):
                     nc.tensor.matmul(
-                        out=ah_ps[:, m, :],
-                        lhsT=wcf_sb[:, c, m:NH:PACK],
+                        out=ah_ps[:, t, :],
+                        lhsT=wcf_sb[:, c, t:NH:PACK],
                         rhs=a_t[:, c, :],
                         start=(c == 0),
                         stop=(c == F_CHUNKS - 1),
                     )
             nc.vector.tensor_tensor(
-                out=atom_x[:].rearrange("x m (j b) -> x m j b", b=MOLS),
-                in0=ah_ps[:].rearrange("x m (b j) -> x m j b", b=MOLS),
-                in1=bias_x[:, H_TILES : 2 * H_TILES].unsqueeze(2).unsqueeze(3).to_broadcast([P, H_TILES, ATOMS, MOLS]),
+                out=atom_x[:].rearrange("p t (j b) -> p t j b", b=MOLS),
+                in0=ah_ps[:].rearrange("p t (b j) -> p t j b", b=MOLS),
+                in1=bcf_x[:].unsqueeze(2).unsqueeze(3).to_broadcast([P, PACK, ATOMS, MOLS]),
                 op=ADD,
             )
 
-        d_grouped, d_codes, gated_tiles, g_codes = {}, {}, {}, {}
+        d_grouped, d_codes, gated_tiles, g_grouped, g_codes, th_tiles = {}, {}, {}, {}, {}, {}
 
-        def run(h):
-            return range(h * HALF, (h + 1) * HALF)
-
-        def transpose_distances(n, h):
-            if h == 0:
-                d_grouped[n] = work.tile([P, D_PASSES, TILES, P, PACK], BF16, align_bytes=64, name="d_grouped")
-            grouped = d_grouped[n]
-            for r in run(h):
-                d_words = d_chunks[n][:, r, :].bitcast(F32)
-                dt_ps = psum.tile([P, D_PASSES, 2, P], F32, tag="dt", name="dt_ps")
+        def transpose_distances(u):
+            grouped = work.tile([P, D_PASSES, TILES, P, PACK], BF16, align_bytes=64, name="d_grouped")
+            d_grouped[u] = grouped
+            for r in range(TILES):
+                d_words = d_units[u][:, r, :].bitcast(F32)
+                dt_ps = psum.tile([P, D_PASSES, 2, P], F32, tag="dt", bufs=DT_BUFS, name="dt_ps")
                 for g in range(D_PASSES):
-                    for u in range(2):
+                    for e in range(2):
                         nc.tensor.transpose(
-                            out=dt_ps[:, g, u, :],
-                            in_=d_words[:, 256 * g + u : 256 * (g + 1) : 2],
+                            out=dt_ps[:, g, e, :],
+                            in_=d_words[:, 256 * g + e : 256 * (g + 1) : 2],
                             identity=ident_f32[:],
                         )
-                nc.scalar.copy(out=grouped[:, :, r].bitcast(F32), in_=dt_ps[:].rearrange("p g u c -> p g c u"))
+                nc.scalar.copy(out=grouped[:, :, r].bitcast(F32), in_=dt_ps[:].rearrange("p g e c -> p g c e"))
 
-        def quantise_distances(n):
+        def quantise_distances(u):
             words = work.tile([P, D_PASSES, PAIRS], U32, align_bytes=64, name="d_words")
             plane = work.tile([P, D_PASSES, PAIRS], U8, align_bytes=64, name="d_plane")
             nc.vector.quantize_mx(
                 out=words[:].rearrange("p g c -> p (g c)").bitcast(FP8X4),
                 scales=plane[:].rearrange("p g c -> p (g c)"),
-                in_=d_grouped[n][:].rearrange("p g r c t -> p (g r c t)"),
+                in_=d_grouped[u][:].rearrange("p g r c t -> p (g r c t)"),
             )
-            d_codes[n] = (words, plane)
+            d_codes[u] = (words, plane)
 
-        def first_matmul(n, h):
-            words, plane = d_codes[n]
-            if h == 0:
-                gated_tiles[n] = work.tile([P, H_TILES, PAIRS], BF16, name="gated")
-            gated = gated_tiles[n]
-            for m in run(h):
-                s1_ps = psum.tile([P, PAIRS], F32, tag="s1", bufs=H_TILES, name="s1_ps")
-                for g in range(D_PASSES):
-                    nc.tensor.matmul_mx(
-                        out=s1_ps[:],
-                        lhsT=wdf_words[:, g, m * P : (m + 1) * P].bitcast(FP8X4),
-                        lhsT_scale=wdf_planes[:, g, m * P : (m + 1) * P],
-                        rhs=words[:, g, :].bitcast(FP8X4),
-                        rhs_scale=plane[:, g, :],
-                        start=(g == 0),
-                        stop=(g == D_PASSES - 1),
+        def first_matmul(u):
+            words, plane = d_codes[u]
+            gated = work.tile([P, PACK, PAIRS], BF16, name="gated")
+            gated_tiles[u] = gated
+            jb = TILES * MOLS
+            for half in range(PACK // 2):
+                s1_ps = psum.tile([P, 2, PAIRS], F32, tag="s1", bufs=S1_BUFS, name="s1_ps")
+                for e in range(2):
+                    t = 2 * half + e
+                    for g in range(D_PASSES):
+                        nc.tensor.matmul_mx(
+                            out=s1_ps[:, e, :],
+                            lhsT=wdf_words[:, g, t * P : (t + 1) * P].bitcast(FP8X4),
+                            lhsT_scale=wdf_planes[:, g, t * P : (t + 1) * P],
+                            rhs=words[:, g, :].bitcast(FP8X4),
+                            rhs_scale=plane[:, g, :],
+                            start=(g == 0),
+                            stop=(g == D_PASSES - 1),
+                        )
+                for e in range(2):
+                    t = 2 * half + e
+                    nc.vector.scalar_tensor_tensor(
+                        out=gated[:, t, :].rearrange("p (q i) -> p q i", i=ATOMS),
+                        in0=s1_ps[:, e, :].rearrange("p (q i) -> p q i", i=ATOMS),
+                        scalar=bdf_x[:, t : t + 1],
+                        in1=atom_x[:, t, u * jb : (u + 1) * jb].unsqueeze(2).to_broadcast([P, jb, ATOMS]),
+                        op0=ADD,
+                        op1=MULT,
                     )
-                jb = TILES * MOLS
-                nc.vector.scalar_tensor_tensor(
-                    out=gated[:, m, :].rearrange("x (q i) -> x q i", i=ATOMS),
-                    in0=s1_ps[:].rearrange("x (q i) -> x q i", i=ATOMS),
-                    scalar=bias_x[:, m : m + 1],
-                    in1=atom_x[:, m, n * jb : (n + 1) * jb].unsqueeze(2).to_broadcast([P, jb, ATOMS]),
-                    op0=ADD,
-                    op1=MULT,
-                )
 
-        def quantise_gated(n, h):
-            cols = HALF * P
-            grouped = work.tile([P, cols, PACK], BF16, align_bytes=64, name="g_grouped")
+        def group_gated(u):
+            grouped = work.tile([P, PAIRS, PACK], BF16, align_bytes=64, name="g_grouped")
+            g_grouped[u] = grouped
             nc.scalar.copy(
                 out=grouped[:].rearrange("p (c i) t -> p c t i", i=4),
-                in_=gated_tiles[n][:, :, h * cols : (h + 1) * cols].rearrange("p t (c i) -> p c t i", i=4),
+                in_=gated_tiles[u][:].rearrange("p t (c i) -> p c t i", i=4),
             )
-            words = work.tile([P, cols], U32, align_bytes=64, name="g_words")
-            plane = work.tile([P, cols], U8, align_bytes=64, name="g_plane")
+
+        def quantise_gated(u):
+            words = work.tile([P, PAIRS], U32, align_bytes=64, name="g_words")
+            plane = work.tile([P, PAIRS], U8, align_bytes=64, name="g_plane")
             nc.vector.quantize_mx(
                 out=words[:].bitcast(FP8X4),
                 scales=plane[:],
-                in_=grouped[:].rearrange("p c t -> p (c t)"),
+                in_=g_grouped[u][:].rearrange("p c t -> p (c t)"),
             )
-            g_codes[n, h] = (words, plane)
+            g_codes[u] = (words, plane)
 
-        def second_matmul(n, h):
-            words, plane = g_codes[n, h]
-            th_sb = th_pool.tile([P, HALF, NF], F32, name="th_sb")
-            for r in run(h):
-                j = n * TILES + r
-                s2_ps = psum.tile([P, NF], F32, tag="s2", name="s2_ps")
+        def second_matmul(u):
+            words, plane = g_codes[u]
+            th_sb = work.tile([P, TILES, NF], F32, name="th_sb")
+            th_tiles[u] = th_sb
+            for r in range(TILES):
+                s2_ps = psum.tile([P, NF], F32, tag="s2", bufs=S2_BUFS, name="s2_ps")
                 nc.tensor.matmul_mx(
                     out=s2_ps[:],
-                    lhsT=words[:, (r % HALF) * P : (r % HALF + 1) * P].bitcast(FP8X4),
-                    lhsT_scale=plane[:, (r % HALF) * P : (r % HALF + 1) * P],
+                    lhsT=words[:, r * P : (r + 1) * P].bitcast(FP8X4),
+                    lhsT_scale=plane[:, r * P : (r + 1) * P],
                     rhs=wfc_words[:].bitcast(FP8X4),
                     rhs_scale=w_planes[:, D_PASSES, :],
                     start=True,
                     stop=True,
                 )
-                nc.scalar.activation(out=th_sb[:, r % HALF, :], in_=s2_ps[:], func=TANH, scale=mask_f32[:, j : j + 1])
-            nc.vector.tensor_tensor(out=sums[:], in0=sums[:], in1=th_sb[:], op=ADD)
+                j = u * TILES + r
+                nc.scalar.activation(out=th_sb[:, r, :], in_=s2_ps[:], func=TANH, scale=mask_f32[:, j : j + 1])
 
-        halves = CHUNKS * (TILES // HALF)
+        def add_up(u):
+            if u < UNITS - TAIL_UNITS:
+                nc.vector.tensor_tensor(out=sums[:], in0=sums[:], in1=th_tiles[u][:], op=ADD)
+                if u == UNITS - TAIL_UNITS - 1:
+                    nc.vector.tensor_tensor(out=sums[:, 0, :], in0=sums[:, 0, :], in1=sums[:, 1, :], op=ADD)
+            else:
+                for r in range(TILES):
+                    nc.vector.tensor_tensor(out=sums[:, 0, :], in0=sums[:, 0, :], in1=th_tiles[u][:, r, :], op=ADD)
 
-        def live(x):
-            return 0 <= x < halves
+        def live(u):
+            return 0 <= u < UNITS
 
-        for k in range(halves + LAG_SECOND):
-            if k % 2 == 0 and live(k + 4):
-                load_distances(k // 2 + 2)
+        small_casts()
+        reorder_words()
+        reorder_scales()
+        transpose_atoms()
+        for k in range(UNITS + LAG_ADD):
             if live(k):
-                transpose_distances(k // 2, k % 2)
-                if k % 2 == 1:
-                    quantise_distances(k // 2)
-            if k == 1:
+                transpose_distances(k)
+            if live(k - LAG_QD):
+                quantise_distances(k - LAG_QD)
+            if k == 0:
                 atom_layer()
             if live(k - LAG_FIRST):
-                first_matmul((k - LAG_FIRST) // 2, (k - LAG_FIRST) % 2)
+                first_matmul(k - LAG_FIRST)
             if live(k - LAG_GROUP):
-                quantise_gated((k - LAG_GROUP) // 2, (k - LAG_GROUP) % 2)
+                group_gated(k - LAG_GROUP)
+            if live(k - LAG_QG):
+                quantise_gated(k - LAG_QG)
             if live(k - LAG_SECOND):
-                second_matmul((k - LAG_SECOND) // 2, (k - LAG_SECOND) % 2)
+                second_matmul(k - LAG_SECOND)
+            if live(k - LAG_ADD):
+                add_up(k - LAG_ADD)
 
-        result = consts.tile([P, NF], F32)
-        nc.vector.tensor_tensor(out=result[:], in0=sums[:, 0, :], in1=sums[:, 1, :], op=ADD)
-        nc.sync.dma_start(out=out.rearrange("b i f -> (b i) f"), in_=result[:])
+        nc.sync.dma_start(out=out.rearrange("b i f -> (b i) f"), in_=sums[:, 0, :])

@@ -25,11 +25,13 @@ F_CHUNKS = NF // P
 TILES = 2
 PAIRS = TILES * P
 UNITS = ATOMS // TILES
-WORK_BUFS = 4
+WORK_BUFS = 7
 DT_BUFS = 2
 S2_BUFS = 2
 S1_BUFS = 4
-TAIL_UNITS = 2
+TAIL_UNITS = 3
+HEADK = 1
+T_UNITS = (11, 12)
 LAG_QD = 0
 LAG_FIRST = 1
 LAG_GROUP = 2
@@ -67,7 +69,11 @@ def tile_dtnnstep_pa_kernel(
 
         def load_distances(u):
             d_sb = d_pool.tile([P, TILES, ND], BF16, name="d_sb")
-            nc.sync.dma_start(out=d_sb[:], in_=d_view[:, u * TILES : (u + 1) * TILES, :])
+            if u == 0:
+                for r in range(TILES):
+                    nc.sync.dma_start(out=d_sb[:, r, :], in_=d_view[:, r, :])
+            else:
+                nc.sync.dma_start(out=d_sb[:], in_=d_view[:, u * TILES : (u + 1) * TILES, :])
             d_units[u] = d_sb
 
         w_planes = consts.tile([P, D_PASSES + 1, NH], U8, align_bytes=64)
@@ -101,26 +107,42 @@ def tile_dtnnstep_pa_kernel(
                     in_=W_fc_scales.bitcast(I32)[0, r:16:4, :],
                 )
 
+        bdf_bf = consts.tile([P, PACK], BF16)
+        bcf_bf = consts.tile([P, PACK], BF16)
+        a_sb = consts.tile([P, NF], BF16)
+        wcf_sb = consts.tile([P, F_CHUNKS, NH], BF16)
+        mask_bf = consts.tile([P, ATOMS], BF16)
+
+        def load_biases():
+            nc.scalar.dma_start(out=bdf_bf[:], in_=b_df.rearrange("(p t) -> p t", t=PACK))
+            nc.scalar.dma_start(out=bcf_bf[:], in_=b_cf.rearrange("(p t) -> p t", t=PACK))
+
+        def load_atoms():
+            nc.sync.dma_start(out=a_sb[:], in_=atom_features.rearrange("b n f -> (b n) f"))
+
+        def load_wcf():
+            for c in range(0, F_CHUNKS, 2):
+                nc.sync.dma_start(
+                    out=wcf_sb[:, c : c + 2, :],
+                    in_=W_cf[c * P : (c + 2) * P, :].rearrange("(c f) h -> f c h", f=P),
+                )
+
+        def load_mask():
+            nc.sync.dma_start(out=mask_bf[:], in_=distance_matrix_mask.rearrange("b i j -> (b i) j"))
+
+        load_biases()
         load_distances(0)
+        load_atoms()
+        load_distances(1)
         load_wdf_words()
         load_wdf_scales()
-        load_distances(1)
+        load_wcf()
         load_distances(2)
+        load_mask()
         load_distances(3)
         load_wfc()
         for u in range(4, UNITS):
             load_distances(u)
-
-        a_sb = consts.tile([P, NF], BF16)
-        nc.scalar.dma_start(out=a_sb[:], in_=atom_features.rearrange("b n f -> (b n) f"))
-        wcf_sb = consts.tile([P, F_CHUNKS, NH], BF16)
-        nc.scalar.dma_start(out=wcf_sb[:], in_=W_cf.rearrange("(c f) h -> f c h", f=P))
-        bdf_bf = consts.tile([P, PACK], BF16)
-        nc.scalar.dma_start(out=bdf_bf[:], in_=b_df.rearrange("(p t) -> p t", t=PACK))
-        bcf_bf = consts.tile([P, PACK], BF16)
-        nc.scalar.dma_start(out=bcf_bf[:], in_=b_cf.rearrange("(p t) -> p t", t=PACK))
-        mask_bf = consts.tile([P, ATOMS], BF16)
-        nc.scalar.dma_start(out=mask_bf[:], in_=distance_matrix_mask.rearrange("b i j -> (b i) j"))
 
         ident_bf = consts.tile([P, P], BF16)
         make_identity(nc, ident_bf[:])
@@ -150,45 +172,53 @@ def tile_dtnnstep_pa_kernel(
                 in_=wdf_raw[:].bitcast(I32).rearrange("p g (y t) -> p g t y", t=PACK),
             )
 
-        def small_casts():
-            nc.vector.memset(sums[:, 1, :], 0.0)
-            nc.vector.tensor_copy(out=sums[:, 0, :], in_=a_sb[:])
+        def cast_biases():
             nc.vector.tensor_copy(out=bdf_x[:], in_=bdf_bf[:])
             nc.vector.tensor_copy(out=bcf_x[:], in_=bcf_bf[:])
+
+        def cast_mask():
             nc.vector.tensor_copy(out=mask_f32[:], in_=mask_bf[:])
 
+        atoms = {}
+
         def transpose_atoms():
-            at_ps = psum.tile([P, F_CHUNKS, P], BF16, tag="s1", bufs=S1_BUFS, name="at_ps")
+            at_ps = psum.tile([P, F_CHUNKS, P], BF16, tag="s2", bufs=S2_BUFS, name="at_ps")
             for c in range(F_CHUNKS):
                 nc.tensor.transpose(out=at_ps[:, c, :], in_=a_sb[:, c * P : (c + 1) * P], identity=ident_bf[:])
             nc.scalar.copy(out=a_t[:], in_=at_ps[:])
 
         def atom_layer():
-            ah_ps = psum.tile([P, PACK, P], F32, tag="s1", bufs=S1_BUFS, name="ah_ps")
-            for t in range(PACK):
-                for c in range(F_CHUNKS):
+            banks = [psum.tile([P, P], F32, tag="s1", bufs=S1_BUFS, name="ah_ps") for t in range(PACK)]
+            atoms["banks"] = banks
+            for c in range(F_CHUNKS):
+                for t in range(PACK):
                     nc.tensor.matmul(
-                        out=ah_ps[:, t, :],
+                        out=banks[t][:],
                         lhsT=wcf_sb[:, c, t:NH:PACK],
                         rhs=a_t[:, c, :],
                         start=(c == 0),
                         stop=(c == F_CHUNKS - 1),
                     )
-            nc.vector.tensor_tensor(
-                out=atom_x[:].rearrange("p t (j b) -> p t j b", b=MOLS),
-                in0=ah_ps[:].rearrange("p t (b j) -> p t j b", b=MOLS),
-                in1=bcf_x[:].unsqueeze(2).unsqueeze(3).to_broadcast([P, PACK, ATOMS, MOLS]),
-                op=ADD,
-            )
+
+        def add_atom_bias():
+            for t in range(PACK):
+                nc.vector.tensor_scalar(
+                    out=atom_x[:, t, :].rearrange("p (j b) -> p j b", b=MOLS),
+                    in0=atoms["banks"][t][:].rearrange("p (b j) -> p j b", b=MOLS),
+                    scalar1=bcf_x[:, t : t + 1],
+                    scalar2=None,
+                    op0=ADD,
+                )
 
         d_grouped, d_codes, gated_tiles, g_grouped, g_codes, th_tiles = {}, {}, {}, {}, {}, {}
+        dt_banks, s1_banks, s2_banks = {}, {}, {}
 
         def transpose_distances(u):
-            grouped = work.tile([P, D_PASSES, TILES, P, PACK], BF16, align_bytes=64, name="d_grouped")
-            d_grouped[u] = grouped
+            dt_banks[u] = []
             for r in range(TILES):
                 d_words = d_units[u][:, r, :].bitcast(F32)
                 dt_ps = psum.tile([P, D_PASSES, 2, P], F32, tag="dt", bufs=DT_BUFS, name="dt_ps")
+                dt_banks[u].append(dt_ps)
                 for g in range(D_PASSES):
                     for e in range(2):
                         nc.tensor.transpose(
@@ -196,7 +226,14 @@ def tile_dtnnstep_pa_kernel(
                             in_=d_words[:, 256 * g + e : 256 * (g + 1) : 2],
                             identity=ident_f32[:],
                         )
-                nc.scalar.copy(out=grouped[:, :, r].bitcast(F32), in_=dt_ps[:].rearrange("p g e c -> p g c e"))
+                if r == 0:
+                    d_grouped[u] = work.tile([P, D_PASSES, TILES, P, PACK], BF16, align_bytes=64, name="d_grouped")
+                copy_distances(u, r)
+
+        def copy_distances(u, r):
+            nc.scalar.copy(
+                out=d_grouped[u][:, :, r].bitcast(F32), in_=dt_banks[u][r][:].rearrange("p g e c -> p g c e")
+            )
 
         def quantise_distances(u):
             words = work.tile([P, D_PASSES, PAIRS], U32, align_bytes=64, name="d_words")
@@ -210,11 +247,10 @@ def tile_dtnnstep_pa_kernel(
 
         def first_matmul(u):
             words, plane = d_codes[u]
-            gated = work.tile([P, PACK, PAIRS], BF16, name="gated")
-            gated_tiles[u] = gated
-            jb = TILES * MOLS
+            s1_banks[u] = []
             for half in range(PACK // 2):
                 s1_ps = psum.tile([P, 2, PAIRS], F32, tag="s1", bufs=S1_BUFS, name="s1_ps")
+                s1_banks[u].append(s1_ps)
                 for e in range(2):
                     t = 2 * half + e
                     for g in range(D_PASSES):
@@ -227,21 +263,33 @@ def tile_dtnnstep_pa_kernel(
                             start=(g == 0),
                             stop=(g == D_PASSES - 1),
                         )
-                for e in range(2):
-                    t = 2 * half + e
-                    nc.vector.scalar_tensor_tensor(
-                        out=gated[:, t, :].rearrange("p (q i) -> p q i", i=ATOMS),
-                        in0=s1_ps[:, e, :].rearrange("p (q i) -> p q i", i=ATOMS),
-                        scalar=bdf_x[:, t : t + 1],
-                        in1=atom_x[:, t, u * jb : (u + 1) * jb].unsqueeze(2).to_broadcast([P, jb, ATOMS]),
-                        op0=ADD,
-                        op1=MULT,
-                    )
+
+        def gate(u):
+            gated = work.tile([P, PACK, PAIRS], BF16, name="gated")
+            gated_tiles[u] = gated
+            jb = TILES * MOLS
+            for t in range(PACK):
+                nc.vector.scalar_tensor_tensor(
+                    out=gated[:, t, :].rearrange("p (q i) -> p q i", i=ATOMS),
+                    in0=s1_banks[u][t // 2][:, t % 2, :].rearrange("p (q i) -> p q i", i=ATOMS),
+                    scalar=bdf_x[:, t : t + 1],
+                    in1=atom_x[:, t, u * jb : (u + 1) * jb].unsqueeze(2).to_broadcast([P, jb, ATOMS]),
+                    op0=ADD,
+                    op1=MULT,
+                )
 
         def group_gated(u):
             grouped = work.tile([P, PAIRS, PACK], BF16, align_bytes=64, name="g_grouped")
             g_grouped[u] = grouped
             nc.scalar.copy(
+                out=grouped[:].rearrange("p (c i) t -> p c t i", i=4),
+                in_=gated_tiles[u][:].rearrange("p t (c i) -> p c t i", i=4),
+            )
+
+        def group_v(u):
+            grouped = work.tile([P, PAIRS, PACK], BF16, align_bytes=64, name="g_grouped")
+            g_grouped[u] = grouped
+            nc.vector.tensor_copy(
                 out=grouped[:].rearrange("p (c i) t -> p c t i", i=4),
                 in_=gated_tiles[u][:].rearrange("p t (c i) -> p c t i", i=4),
             )
@@ -258,10 +306,10 @@ def tile_dtnnstep_pa_kernel(
 
         def second_matmul(u):
             words, plane = g_codes[u]
-            th_sb = work.tile([P, TILES, NF], F32, name="th_sb")
-            th_tiles[u] = th_sb
+            s2_banks[u] = []
             for r in range(TILES):
                 s2_ps = psum.tile([P, NF], F32, tag="s2", bufs=S2_BUFS, name="s2_ps")
+                s2_banks[u].append(s2_ps)
                 nc.tensor.matmul_mx(
                     out=s2_ps[:],
                     lhsT=words[:, r * P : (r + 1) * P].bitcast(FP8X4),
@@ -271,14 +319,54 @@ def tile_dtnnstep_pa_kernel(
                     start=True,
                     stop=True,
                 )
+
+        def squash(u):
+            th_sb = sums if u == 0 else work.tile([P, TILES, NF], F32, name="th_sb")
+            th_tiles[u] = th_sb
+            for r in range(TILES):
                 j = u * TILES + r
-                nc.scalar.activation(out=th_sb[:, r, :], in_=s2_ps[:], func=TANH, scale=mask_f32[:, j : j + 1])
+                nc.scalar.activation(out=th_sb[:, r, :], in_=s2_banks[u][r][:], func=TANH, scale=mask_f32[:, j : j + 1])
+
+        t_sum = {}
+
+        def start_tensor_sum0():
+            acc = psum.tile([P, F_CHUNKS, P], F32, tag="dt", bufs=DT_BUFS, name="acc_ps")
+            tiles = [(u, r) for u in T_UNITS for r in range(TILES)]
+            for c in range(F_CHUNKS):
+                for n, (u, r) in enumerate(tiles):
+                    nc.tensor.matmul(
+                        out=acc[:, c, :],
+                        lhsT=th_tiles[u][:, r, c * P : (c + 1) * P],
+                        rhs=ident_f32[:],
+                        is_transpose=True,
+                        start=(n == 0),
+                        stop=(n == len(tiles) - 1),
+                    )
+            t_sum["acc"] = acc
+
+        def start_tensor_sum1():
+            acc_sb = consts.tile([P, F_CHUNKS, P], F32, name="acc_sb")
+            nc.scalar.copy(out=acc_sb[:], in_=t_sum["acc"][:])
+            t_sum["sb"] = acc_sb
+
+        def turn_tensor_sum():
+            back = psum.tile([P, NF], F32, tag="dt", bufs=DT_BUFS, name="back_ps")
+            for c in range(F_CHUNKS):
+                nc.tensor.transpose(out=back[:, c * P : (c + 1) * P], in_=t_sum["sb"][:, c, :], identity=ident_f32[:])
+            t_sum["back"] = back
+
+        def join_sums():
+            nc.vector.tensor_tensor(out=sums[:, 0, :], in0=sums[:, 0, :], in1=a_sb[:], op=ADD)
+            nc.vector.tensor_tensor(out=sums[:, 0, :], in0=sums[:, 0, :], in1=sums[:, 1, :], op=ADD)
+
+        def add_tensor_sum():
+            nc.vector.tensor_tensor(out=sums[:, 0, :], in0=sums[:, 0, :], in1=t_sum["back"][:], op=ADD)
 
         def add_up(u):
+            if u == 0 or u in T_UNITS:
+                return
             if u < UNITS - TAIL_UNITS:
                 nc.vector.tensor_tensor(out=sums[:], in0=sums[:], in1=th_tiles[u][:], op=ADD)
-                if u == UNITS - TAIL_UNITS - 1:
-                    nc.vector.tensor_tensor(out=sums[:, 0, :], in0=sums[:, 0, :], in1=sums[:, 1, :], op=ADD)
             else:
                 for r in range(TILES):
                     nc.vector.tensor_tensor(out=sums[:, 0, :], in0=sums[:, 0, :], in1=th_tiles[u][:, r, :], op=ADD)
@@ -286,26 +374,58 @@ def tile_dtnnstep_pa_kernel(
         def live(u):
             return 0 <= u < UNITS
 
-        small_casts()
+        cast_biases()
+        transpose_distances(0)
+        quantise_distances(0)
+        transpose_atoms()
+        transpose_distances(1)
         reorder_words()
         reorder_scales()
-        transpose_atoms()
-        for k in range(UNITS + LAG_ADD):
-            if live(k):
-                transpose_distances(k)
-            if live(k - LAG_QD):
-                quantise_distances(k - LAG_QD)
-            if k == 0:
-                atom_layer()
-            if live(k - LAG_FIRST):
-                first_matmul(k - LAG_FIRST)
-            if live(k - LAG_GROUP):
-                group_gated(k - LAG_GROUP)
-            if live(k - LAG_QG):
-                quantise_gated(k - LAG_QG)
-            if live(k - LAG_SECOND):
-                second_matmul(k - LAG_SECOND)
-            if live(k - LAG_ADD):
-                add_up(k - LAG_ADD)
+        quantise_distances(1)
+        atom_layer()
+        add_atom_bias()
+        cast_mask()
+        transpose_distances(2)
+        first_matmul(0)
+        gate(0)
+        quantise_distances(2)
+        first_matmul(1)
+        gate(1)
+        group_gated(0)
+        quantise_gated(0)
+
+        for k in range(3, UNITS):
+            transpose_distances(k)
+            quantise_distances(k)
+            first_matmul(k - 1)
+            gate(k - 1)
+            if live(k - 2):
+                group_gated(k - 2)
+                quantise_gated(k - 2)
+            if live(k - 3):
+                second_matmul(k - 3)
+                squash(k - 3)
+                if k - 3 <= 10:
+                    add_up(k - 3)
+        first_matmul(15)
+        gate(15)
+        group_gated(14)
+        quantise_gated(14)
+        second_matmul(13)
+        start_tensor_sum0()
+        group_gated(15)
+        squash(13)
+        join_sums()
+        quantise_gated(15)
+        start_tensor_sum1()
+        second_matmul(14)
+        turn_tensor_sum()
+        add_up(13)
+        squash(14)
+        second_matmul(15)
+        squash(15)
+        add_up(14)
+        add_tensor_sum()
+        add_up(15)
 
         nc.sync.dma_start(out=out.rearrange("b i f -> (b i) f"), in_=sums[:, 0, :])

@@ -29,9 +29,9 @@ WORK_BUFS = 7
 DT_BUFS = 2
 S2_BUFS = 2
 S1_BUFS = 4
-TAIL_UNITS = 3
+TAIL_UNITS = 2
 HEADK = 1
-T_UNITS = (11, 12)
+T_UNITS = ()
 LAG_QD = 0
 LAG_FIRST = 1
 LAG_GROUP = 2
@@ -355,21 +355,32 @@ def tile_dtnnstep_pa_kernel(
                 nc.tensor.transpose(out=back[:, c * P : (c + 1) * P], in_=t_sum["sb"][:, c, :], identity=ident_f32[:])
             t_sum["back"] = back
 
+        def halves():
+            return [slice(h * NF // 2, (h + 1) * NF // 2) for h in range(2)]
+
         def join_sums():
-            nc.vector.tensor_tensor(out=sums[:, 0, :], in0=sums[:, 0, :], in1=a_sb[:], op=ADD)
-            nc.vector.tensor_tensor(out=sums[:, 0, :], in0=sums[:, 0, :], in1=sums[:, 1, :], op=ADD)
+            for h in halves():
+                nc.vector.tensor_tensor(out=sums[:, 0, h], in0=sums[:, 0, h], in1=sums[:, 1, h], op=ADD)
 
         def add_tensor_sum():
-            nc.vector.tensor_tensor(out=sums[:, 0, :], in0=sums[:, 0, :], in1=t_sum["back"][:], op=ADD)
+            for h in halves():
+                nc.vector.tensor_tensor(out=sums[:, 0, h], in0=sums[:, 0, h], in1=t_sum["back"][:, h], op=ADD)
+
+        def add_tile(u, r):
+            for h in halves():
+                nc.vector.tensor_tensor(out=sums[:, 0, h], in0=sums[:, 0, h], in1=th_tiles[u][:, r, h], op=ADD)
+
+        def add_tiles(u):
+            for r in range(TILES):
+                add_tile(u, r)
 
         def add_up(u):
-            if u == 0 or u in T_UNITS:
+            if u in T_UNITS:
                 return
-            if u < UNITS - TAIL_UNITS:
-                nc.vector.tensor_tensor(out=sums[:], in0=sums[:], in1=th_tiles[u][:], op=ADD)
+            if u == 0:
+                nc.vector.tensor_tensor(out=sums[:, 0, :], in0=sums[:, 0, :], in1=a_sb[:], op=ADD)
             else:
-                for r in range(TILES):
-                    nc.vector.tensor_tensor(out=sums[:, 0, :], in0=sums[:, 0, :], in1=th_tiles[u][:, r, :], op=ADD)
+                nc.vector.tensor_tensor(out=sums[:], in0=sums[:], in1=th_tiles[u][:], op=ADD)
 
         def live(u):
             return 0 <= u < UNITS
@@ -384,7 +395,6 @@ def tile_dtnnstep_pa_kernel(
         quantise_distances(1)
         atom_layer()
         add_atom_bias()
-        cast_mask()
         transpose_distances(2)
         first_matmul(0)
         gate(0)
@@ -394,38 +404,35 @@ def tile_dtnnstep_pa_kernel(
         group_gated(0)
         quantise_gated(0)
 
+        cast_mask()
         for k in range(3, UNITS):
             transpose_distances(k)
             quantise_distances(k)
             first_matmul(k - 1)
             gate(k - 1)
-            if live(k - 2):
-                group_gated(k - 2)
-                quantise_gated(k - 2)
+            group_gated(k - 2)
+            quantise_gated(k - 2)
             if live(k - 3):
                 second_matmul(k - 3)
                 squash(k - 3)
-                if k - 3 <= 10:
+                if k - 3 <= 12:
                     add_up(k - 3)
         first_matmul(15)
         gate(15)
         group_gated(14)
         quantise_gated(14)
         second_matmul(13)
-        start_tensor_sum0()
-        group_gated(15)
         squash(13)
-        join_sums()
-        quantise_gated(15)
-        start_tensor_sum1()
-        second_matmul(14)
-        turn_tensor_sum()
+        group_gated(15)
         add_up(13)
+        quantise_gated(15)
+        second_matmul(14)
         squash(14)
+        join_sums()
         second_matmul(15)
         squash(15)
-        add_up(14)
-        add_tensor_sum()
-        add_up(15)
+        add_tiles(14)
+        add_tiles(15)
 
-        nc.sync.dma_start(out=out.rearrange("b i f -> (b i) f"), in_=sums[:, 0, :])
+        for h in halves():
+            nc.sync.dma_start(out=out.rearrange("b i f -> (b i) f")[:, h], in_=sums[:, 0, h])

@@ -172,6 +172,11 @@ def tile_dtnnstep_pa_kernel(
                 in_=wdf_raw[:].bitcast(I32).rearrange("p g (y t) -> p g t y", t=PACK),
             )
 
+        def keep_warm(count):
+            warm_ps = psum.tile([P, P], F32, tag="s2", bufs=S2_BUFS, name="warm_ps")
+            for n in range(count):
+                nc.tensor.matmul(out=warm_ps[:], lhsT=ident_bf[:], rhs=ident_bf[:], start=True, stop=True)
+
         def cast_biases():
             nc.vector.tensor_copy(out=bdf_x[:], in_=bdf_bf[:])
             nc.vector.tensor_copy(out=bcf_x[:], in_=bcf_bf[:])
@@ -286,6 +291,75 @@ def tile_dtnnstep_pa_kernel(
                 in_=gated_tiles[u][:].rearrange("p t (c i) -> p c t i", i=4),
             )
 
+        def first_matmul_tile(u, r):
+            words, plane = d_codes[u]
+            s1_ps = psum.tile([P, PACK, P], F32, tag="s1", bufs=S1_BUFS, name="s1_ps")
+            s1_banks[u, r] = s1_ps
+            c = slice(r * P, (r + 1) * P)
+            for t in range(PACK):
+                for g in range(D_PASSES):
+                    nc.tensor.matmul_mx(
+                        out=s1_ps[:, t, :],
+                        lhsT=wdf_words[:, g, t * P : (t + 1) * P].bitcast(FP8X4),
+                        lhsT_scale=wdf_planes[:, g, t * P : (t + 1) * P],
+                        rhs=words[:, g, c].bitcast(FP8X4),
+                        rhs_scale=plane[:, g, c],
+                        start=(g == 0),
+                        stop=(g == D_PASSES - 1),
+                    )
+
+        def gate_tile(u, r):
+            gated = work.tile([P, PACK, P], BF16, name="gated_t")
+            gated_tiles[u, r] = gated
+            j = u * TILES + r
+            for t in range(PACK):
+                nc.vector.scalar_tensor_tensor(
+                    out=gated[:, t, :].rearrange("p (q i) -> p q i", i=ATOMS),
+                    in0=s1_banks[u, r][:, t, :].rearrange("p (q i) -> p q i", i=ATOMS),
+                    scalar=bdf_x[:, t : t + 1],
+                    in1=atom_x[:, t, j * MOLS : (j + 1) * MOLS].unsqueeze(2).to_broadcast([P, MOLS, ATOMS]),
+                    op0=ADD,
+                    op1=MULT,
+                )
+
+        def group_tile(u, r):
+            grouped = work.tile([P, P, PACK], BF16, align_bytes=64, name="g_grouped_t")
+            g_grouped[u, r] = grouped
+            nc.scalar.copy(
+                out=grouped[:].rearrange("p (c i) t -> p c t i", i=4),
+                in_=gated_tiles[u, r][:].rearrange("p t (c i) -> p c t i", i=4),
+            )
+
+        def quantise_tile(u, r):
+            words = work.tile([P, P], U32, align_bytes=64, name="g_words_t")
+            plane = work.tile([P, P], U8, align_bytes=64, name="g_plane_t")
+            nc.vector.quantize_mx(
+                out=words[:].bitcast(FP8X4), scales=plane[:], in_=g_grouped[u, r][:].rearrange("p c t -> p (c t)")
+            )
+            g_codes[u, r] = (words, plane)
+
+        def second_matmul_tile(u, r):
+            words, plane = g_codes[u, r]
+            s2_ps = psum.tile([P, NF], F32, tag="s2", bufs=S2_BUFS, name="s2_ps")
+            s2_banks.setdefault(u, []).append(s2_ps)
+            nc.tensor.matmul_mx(
+                out=s2_ps[:],
+                lhsT=words[:].bitcast(FP8X4),
+                lhsT_scale=plane[:],
+                rhs=wfc_words[:].bitcast(FP8X4),
+                rhs_scale=w_planes[:, D_PASSES, :],
+                start=True,
+                stop=True,
+            )
+
+        def squash_tile(u, r):
+            if r == 0:
+                th_tiles[u] = work.tile([P, TILES, NF], F32, name="th_sb")
+            j = u * TILES + r
+            nc.scalar.activation(
+                out=th_tiles[u][:, r, :], in_=s2_banks[u][r][:], func=TANH, scale=mask_f32[:, j : j + 1]
+            )
+
         def group_v(u):
             grouped = work.tile([P, PAIRS, PACK], BF16, align_bytes=64, name="g_grouped")
             g_grouped[u] = grouped
@@ -349,6 +423,23 @@ def tile_dtnnstep_pa_kernel(
             nc.scalar.copy(out=acc_sb[:], in_=t_sum["acc"][:])
             t_sum["sb"] = acc_sb
 
+        def tensor_add(u):
+            first = u == T_UNITS[0]
+            last = u == T_UNITS[-1]
+            if first:
+                t_sum["acc"] = psum.tile([P, F_CHUNKS, P], F32, tag="acc", bufs=1, name="acc_ps")
+            acc = t_sum["acc"]
+            for r in range(TILES):
+                for c in range(F_CHUNKS):
+                    nc.tensor.matmul(
+                        out=acc[:, c, :],
+                        lhsT=th_tiles[u][:, r, c * P : (c + 1) * P],
+                        rhs=ident_f32[:],
+                        is_transpose=True,
+                        start=(first and r == 0 and c == 0),
+                        stop=(last and r == TILES - 1 and c == F_CHUNKS - 1),
+                    )
+
         def turn_tensor_sum():
             back = psum.tile([P, NF], F32, tag="dt", bufs=DT_BUFS, name="back_ps")
             for c in range(F_CHUNKS):
@@ -386,10 +477,13 @@ def tile_dtnnstep_pa_kernel(
             return 0 <= u < UNITS
 
         cast_biases()
+        keep_warm(12)
         transpose_distances(0)
         quantise_distances(0)
         transpose_atoms()
+        keep_warm(6)
         transpose_distances(1)
+        keep_warm(6)
         reorder_words()
         reorder_scales()
         quantise_distances(1)
@@ -403,7 +497,6 @@ def tile_dtnnstep_pa_kernel(
         gate(1)
         group_gated(0)
         quantise_gated(0)
-
         cast_mask()
         for k in range(3, UNITS):
             transpose_distances(k)

@@ -12,6 +12,7 @@ FP8X4 = mybir.dt.float8_e4m3fn_x4
 ADD = mybir.AluOpType.add
 MULT = mybir.AluOpType.mult
 TANH = mybir.ActivationFunctionType.Tanh
+IDENTITY = mybir.ActivationFunctionType.Identity
 
 P = 128
 PACK = 4
@@ -193,7 +194,13 @@ def tile_dtnnstep_pa_kernel(
             nc.scalar.copy(out=a_t[:], in_=at_ps[:])
 
         def atom_layer():
-            banks = [psum.tile([P, P], F32, tag="s1", bufs=S1_BUFS, name="ah_ps") for t in range(PACK)]
+            banks = []
+            for t in range(PACK):
+                if t < PACK // 2:
+                    ah_ps = psum.tile([P, P], F32, tag="s1", bufs=S1_BUFS, name="ah_ps")
+                else:
+                    ah_ps = psum.tile([P, P], F32, tag="s2", bufs=S2_BUFS, name="ah_ps")
+                banks.append(ah_ps)
             atoms["banks"] = banks
             for c in range(F_CHUNKS):
                 for t in range(PACK):
@@ -283,6 +290,37 @@ def tile_dtnnstep_pa_kernel(
                     op1=MULT,
                 )
 
+        def gate_runs(u, runs):
+            gated = work.tile([P, PACK, PAIRS], BF16, name="gated")
+            gated_tiles[u] = gated
+            jb = TILES * MOLS
+            for t in runs:
+                nc.vector.scalar_tensor_tensor(
+                    out=gated[:, t, :].rearrange("p (q i) -> p q i", i=ATOMS),
+                    in0=s1_banks[u][t // 2][:, t % 2, :].rearrange("p (q i) -> p q i", i=ATOMS),
+                    scalar=bdf_x[:, t : t + 1],
+                    in1=atom_x[:, t, u * jb : (u + 1) * jb].unsqueeze(2).to_broadcast([P, jb, ATOMS]),
+                    op0=ADD,
+                    op1=MULT,
+                )
+
+        def gate_scalar(u, t):
+            jb = TILES * MOLS
+            for q in range(jb):
+                c = u * jb + q
+                nc.scalar.activation(
+                    out=gated_tiles[u][:, t, q * ATOMS : (q + 1) * ATOMS],
+                    in_=s1_banks[u][t // 2][:, t % 2, q * ATOMS : (q + 1) * ATOMS],
+                    func=IDENTITY,
+                    scale=atom_x[:, t, c : c + 1],
+                    bias=shift_x[:, t, c : c + 1],
+                )
+
+        def make_shift(t):
+            nc.vector.tensor_scalar(out=shift_x[:, t, :], in0=atom_x[:, t, :], scalar1=bdf_x[:, t : t + 1], scalar2=None, op0=MULT)
+
+        shift_x = consts.tile([P, PACK, ATOMS * MOLS], F32)
+
         def group_gated(u):
             grouped = work.tile([P, PAIRS, PACK], BF16, align_bytes=64, name="g_grouped")
             g_grouped[u] = grouped
@@ -358,6 +396,22 @@ def tile_dtnnstep_pa_kernel(
             j = u * TILES + r
             nc.scalar.activation(
                 out=th_tiles[u][:, r, :], in_=s2_banks[u][r][:], func=TANH, scale=mask_f32[:, j : j + 1]
+            )
+
+        def open_gpsimd(u):
+            grouped = work.tile([P, PAIRS, PACK], BF16, align_bytes=64, name="g_grouped")
+            g_grouped[u] = grouped
+            nc.vector.memset(grouped[:, 0, :], 0.0)
+
+        def group_g(u):
+            grouped = g_grouped[u]
+            nc.gpsimd.tensor_scalar(
+                out=grouped[:].rearrange("p (c i) t -> p c t i", i=4),
+                in0=gated_tiles[u][:].rearrange("p t (c i) -> p c t i", i=4),
+                scalar1=1.0,
+                scalar2=0.0,
+                op0=MULT,
+                op1=ADD,
             )
 
         def group_v(u):
@@ -499,11 +553,16 @@ def tile_dtnnstep_pa_kernel(
         quantise_gated(0)
         cast_mask()
         for k in range(3, UNITS):
+            if k - 2 in range(1, 14):
+                open_gpsimd(k - 2)
             transpose_distances(k)
             quantise_distances(k)
+            if k - 2 in range(1, 14):
+                group_g(k - 2)
             first_matmul(k - 1)
             gate(k - 1)
-            group_gated(k - 2)
+            if k - 2 not in range(1, 14):
+                group_gated(k - 2)
             quantise_gated(k - 2)
             if live(k - 3):
                 second_matmul(k - 3)

@@ -414,6 +414,14 @@ def tile_dtnnstep_pa_kernel(
                 op1=ADD,
             )
 
+        def split_group(u, pairs, engine):
+            dst = g_grouped[u][:, pairs, :].rearrange("p (c i) t -> p c t i", i=4)
+            src = gated_tiles[u][:, :, pairs].rearrange("p t (c i) -> p c t i", i=4)
+            if engine == "gpsimd":
+                nc.gpsimd.tensor_scalar(out=dst, in0=src, scalar1=1.0, scalar2=0.0, op0=MULT, op1=ADD)
+            else:
+                nc.scalar.copy(out=dst, in_=src)
+
         def group_v(u):
             grouped = work.tile([P, PAIRS, PACK], BF16, align_bytes=64, name="g_grouped")
             g_grouped[u] = grouped
@@ -558,10 +566,12 @@ def tile_dtnnstep_pa_kernel(
             transpose_distances(k)
             quantise_distances(k)
             if k - 2 in range(1, 14):
-                group_g(k - 2)
+                split_group(k - 2, slice(0, 128), "gpsimd")
             first_matmul(k - 1)
             gate(k - 1)
-            if k - 2 not in range(1, 14):
+            if k - 2 in range(1, 14):
+                split_group(k - 2, slice(128, PAIRS), "scalar")
+            else:
                 group_gated(k - 2)
             quantise_gated(k - 2)
             if live(k - 3):

@@ -33,6 +33,9 @@ S1_BUFS = 4
 TAIL_UNITS = 2
 HEADK = 1
 T_UNITS = ()
+T_FROM = 0
+G_UNITS = range(1, 12)
+G_COLS = 256
 LAG_QD = 0
 LAG_FIRST = 1
 LAG_GROUP = 2
@@ -491,14 +494,14 @@ def tile_dtnnstep_pa_kernel(
             if first:
                 t_sum["acc"] = psum.tile([P, F_CHUNKS, P], F32, tag="acc", bufs=1, name="acc_ps")
             acc = t_sum["acc"]
-            for r in range(TILES):
+            for r in range(T_FROM, TILES):
                 for c in range(F_CHUNKS):
                     nc.tensor.matmul(
                         out=acc[:, c, :],
                         lhsT=th_tiles[u][:, r, c * P : (c + 1) * P],
                         rhs=ident_f32[:],
                         is_transpose=True,
-                        start=(first and r == 0 and c == 0),
+                        start=(first and r == T_FROM and c == 0),
                         stop=(last and r == TILES - 1 and c == F_CHUNKS - 1),
                     )
 
@@ -529,11 +532,21 @@ def tile_dtnnstep_pa_kernel(
 
         def add_up(u):
             if u in T_UNITS:
+                for r in range(T_FROM):
+                    nc.vector.tensor_tensor(out=sums[:, r, :], in0=sums[:, r, :], in1=th_tiles[u][:, r, :], op=ADD)
                 return
             if u == 0:
                 nc.vector.tensor_tensor(out=sums[:, 0, :], in0=sums[:, 0, :], in1=a_sb[:], op=ADD)
+            elif u in G_UNITS:
+                flat = sums[:].rearrange("p r f -> p (r f)")[:, 0 : TILES * NF - G_COLS]
+                new = th_tiles[u][:].rearrange("p r f -> p (r f)")[:, 0 : TILES * NF - G_COLS]
+                nc.vector.tensor_tensor(out=flat, in0=flat, in1=new, op=ADD)
             else:
                 nc.vector.tensor_tensor(out=sums[:], in0=sums[:], in1=th_tiles[u][:], op=ADD)
+
+        def add_gpsimd(u):
+            mine = sums[:, 1, NF - G_COLS : NF]
+            nc.gpsimd.tensor_tensor(out=mine, in0=mine, in1=th_tiles[u][:, 1, NF - G_COLS : NF], op=ADD)
 
         def live(u):
             return 0 <= u < UNITS
@@ -563,22 +576,30 @@ def tile_dtnnstep_pa_kernel(
         for k in range(3, UNITS):
             if k - 2 in range(1, 14):
                 open_gpsimd(k - 2)
-            transpose_distances(k)
-            quantise_distances(k)
+            if live(k - 0):
+                transpose_distances(k - 0)
+            if k - 4 in T_UNITS:
+                tensor_add(k - 4)
+            if live(k - 0):
+                quantise_distances(k - 0)
             if k - 2 in range(1, 14):
-                split_group(k - 2, slice(0, 128), "gpsimd")
+                split_group(k - 2, slice(0, 64), "gpsimd")
+            if k - 4 in G_UNITS:
+                add_gpsimd(k - 4)
             first_matmul(k - 1)
             gate(k - 1)
             if k - 2 in range(1, 14):
-                split_group(k - 2, slice(128, PAIRS), "scalar")
+                split_group(k - 2, slice(64, PAIRS), "scalar")
             else:
                 group_gated(k - 2)
             quantise_gated(k - 2)
             if live(k - 3):
                 second_matmul(k - 3)
+            if live(k - 3):
                 squash(k - 3)
-                if k - 3 <= 12:
-                    add_up(k - 3)
+            if live(k - 3) and k - 3 <= 12:
+                add_up(k - 3)
+
         first_matmul(15)
         gate(15)
         group_gated(14)

from contextlib import ExitStack

import concourse.mybir as mybir
from concourse.masks import make_identity

F32 = mybir.dt.float32
BF16 = mybir.dt.bfloat16
I32 = mybir.dt.int32
U32 = mybir.dt.uint32
U8 = mybir.dt.uint8
FP8X4 = mybir.dt.float8_e4m3fn_x4
ADD = mybir.AluOpType.add
MULT = mybir.AluOpType.mult
TANH = mybir.ActivationFunctionType.Tanh
IDENTITY = mybir.ActivationFunctionType.Identity

P = 128
PACK = 4
MOLS = 4
ATOMS = 32
NF = 512
ND = 1024
NH = 512
D_PASSES = ND // (P * PACK)
F_CHUNKS = NF // P
TILES = 2
PAIRS = TILES * P
UNITS = ATOMS // TILES
WORK_BUFS = 7
DT_BUFS = 2
S2_BUFS = 2
S1_BUFS = 4
TAIL_UNITS = 2
HEADK = 1
T_UNITS = ()
T_FROM = 0
G_UNITS = range(1, 12)
G_COLS = 256
LAG_QD = 0
LAG_FIRST = 1
LAG_GROUP = 2
LAG_QG = 2
LAG_SECOND = 3
LAG_ADD = 3

FLOPS = 2 * MOLS * ATOMS * ATOMS * (ND * NH + NH * NF) + 2 * MOLS * ATOMS * NF * NH


def tile_dtnnstep_pa_kernel(
    tc,
    atom_features,
    distance_matrix,
    distance_matrix_mask,
    W_cf,
    W_df_words,
    W_df_scales,
    W_fc_words,
    W_fc_scales,
    b_cf,
    b_df,
    out,
):
    nc = tc.nc
    with ExitStack() as stack:
        stack.enter_context(tc.manual_schedule())
        consts = stack.enter_context(tc.tile_pool(name="consts", bufs=1))
        d_pool = stack.enter_context(tc.tile_pool(name="d_pool", bufs=UNITS))
        work = stack.enter_context(tc.tile_pool(name="work", bufs=WORK_BUFS))
        psum = stack.enter_context(tc.psum_pool(name="psum", bufs=2))

        d_view = distance_matrix.rearrange("b i j k -> (b i) j k")
        d_units = {}

        def load_distances(u):
            d_sb = d_pool.tile([P, TILES, ND], BF16, name="d_sb")
            if u == 0:
                for r in range(TILES):
                    nc.sync.dma_start(out=d_sb[:, r, :], in_=d_view[:, r, :])
            else:
                nc.sync.dma_start(out=d_sb[:], in_=d_view[:, u * TILES : (u + 1) * TILES, :])
            d_units[u] = d_sb

        w_planes = consts.tile([P, D_PASSES + 1, NH], U8, align_bytes=64)
        nc.vector.memset(w_planes[:].bitcast(I32), 0)
        wdf_raw = consts.tile([P, D_PASSES, NH], U32, align_bytes=64)
        wdf_words = consts.tile([P, D_PASSES, NH], U32, align_bytes=64)
        wdf_planes = consts.tile([P, D_PASSES, NH], U8, align_bytes=64)
        wfc_words = consts.tile([P, NF], U32, align_bytes=64)

        def load_wdf_scales():
            for r in range(4):
                nc.sync.dma_start(
                    out=w_planes[r:P:32, 0:D_PASSES, :].bitcast(I32),
                    in_=W_df_scales.bitcast(I32)[:, r:16:4, :].rearrange("g q n -> q g n"),
                )

        def load_wdf_words():
            nc.sync.dma_start(
                out=wdf_raw[:].bitcast(I32),
                in_=W_df_words.rearrange("g p n t -> p g (n t)").bitcast(I32),
            )

        def load_wfc():
            nc.sync.dma_start(
                out=wfc_words[:].bitcast(I32),
                in_=W_fc_words.rearrange("g p n t -> p (g n t)").bitcast(I32),
            )
            for r in range(4):
                nc.sync.dma_start(
                    out=w_planes[r:P:32, D_PASSES, :].bitcast(I32),
                    in_=W_fc_scales.bitcast(I32)[0, r:16:4, :],
                )

        bdf_bf = consts.tile([P, PACK], BF16)
        bcf_bf = consts.tile([P, PACK], BF16)
        a_sb = consts.tile([P, NF], BF16)
        wcf_sb = consts.tile([P, F_CHUNKS, NH], BF16)
        mask_bf = consts.tile([P, ATOMS], BF16)

        def load_biases():
            nc.scalar.dma_start(out=bdf_bf[:], in_=b_df.rearrange("(p t) -> p t", t=PACK))
            nc.scalar.dma_start(out=bcf_bf[:], in_=b_cf.rearrange("(p t) -> p t", t=PACK))

        def load_atoms():
            nc.sync.dma_start(out=a_sb[:], in_=atom_features.rearrange("b n f -> (b n) f"))

        def load_wcf():
            for c in range(0, F_CHUNKS, 2):
                nc.sync.dma_start(
                    out=wcf_sb[:, c : c + 2, :],
                    in_=W_cf[c * P : (c + 2) * P, :].rearrange("(c f) h -> f c h", f=P),
                )

        def load_mask():
            nc.sync.dma_start(out=mask_bf[:], in_=distance_matrix_mask.rearrange("b i j -> (b i) j"))

        load_biases()
        load_distances(0)
        load_atoms()
        load_distances(1)
        load_wdf_words()
        load_wdf_scales()
        load_wcf()
        load_distances(2)
        load_mask()
        load_distances(3)
        load_wfc()
        for u in range(4, UNITS):
            load_distances(u)

        ident_bf = consts.tile([P, P], BF16)
        make_identity(nc, ident_bf[:])
        ident_f32 = consts.tile([P, P], F32)
        make_identity(nc, ident_f32[:])

        warm = consts.tile([P, 1], F32)
        nc.vector.memset(warm[:], 0.0)
        nc.scalar.activation(out=warm[:], in_=warm[:], func=TANH)

        mask_f32 = consts.tile([P, ATOMS], F32)
        sums = consts.tile([P, TILES, NF], F32)
        bdf_x = consts.tile([P, PACK], F32)
        bcf_x = consts.tile([P, PACK], F32)
        atom_x = consts.tile([P, PACK, ATOMS * MOLS], F32)
        a_t = consts.tile([P, F_CHUNKS, P], BF16)

        def reorder_scales():
            nc.vector.tensor_copy(
                out=wdf_planes[:].rearrange("p g (t y) -> p g t y", t=PACK),
                in_=w_planes[:, 0:D_PASSES, :].rearrange("p g (y t) -> p g t y", t=PACK),
            )

        def reorder_words():
            nc.vector.tensor_copy(
                out=wdf_words[:].bitcast(I32).rearrange("p g (t y) -> p g t y", t=PACK),
                in_=wdf_raw[:].bitcast(I32).rearrange("p g (y t) -> p g t y", t=PACK),
            )

        def keep_warm(count):
            warm_ps = psum.tile([P, P], F32, tag="s2", bufs=S2_BUFS, name="warm_ps")
            for n in range(count):
                nc.tensor.matmul(out=warm_ps[:], lhsT=ident_bf[:], rhs=ident_bf[:], start=True, stop=True)

        def cast_biases():
            nc.vector.tensor_copy(out=bdf_x[:], in_=bdf_bf[:])
            nc.vector.tensor_copy(out=bcf_x[:], in_=bcf_bf[:])

        def cast_mask():
            nc.vector.tensor_copy(out=mask_f32[:], in_=mask_bf[:])

        atoms = {}

        def transpose_atoms():
            at_ps = psum.tile([P, F_CHUNKS, P], BF16, tag="s2", bufs=S2_BUFS, name="at_ps")
            for c in range(F_CHUNKS):
                nc.tensor.transpose(out=at_ps[:, c, :], in_=a_sb[:, c * P : (c + 1) * P], identity=ident_bf[:])
            nc.scalar.copy(out=a_t[:], in_=at_ps[:])

        def atom_layer():
            banks = []
            for t in range(PACK):
                if t < PACK // 2:
                    ah_ps = psum.tile([P, P], F32, tag="s1", bufs=S1_BUFS, name="ah_ps")
                else:
                    ah_ps = psum.tile([P, P], F32, tag="s2", bufs=S2_BUFS, name="ah_ps")
                banks.append(ah_ps)
            atoms["banks"] = banks
            for c in range(F_CHUNKS):
                for t in range(PACK):
                    nc.tensor.matmul(
                        out=banks[t][:],
                        lhsT=wcf_sb[:, c, t:NH:PACK],
                        rhs=a_t[:, c, :],
                        start=(c == 0),
                        stop=(c == F_CHUNKS - 1),
                    )

        def add_atom_bias():
            for t in range(PACK):
                nc.vector.tensor_scalar(
                    out=atom_x[:, t, :].rearrange("p (j b) -> p j b", b=MOLS),
                    in0=atoms["banks"][t][:].rearrange("p (b j) -> p j b", b=MOLS),
                    scalar1=bcf_x[:, t : t + 1],
                    scalar2=None,
                    op0=ADD,
                )

        d_grouped, d_codes, gated_tiles, g_grouped, g_codes, th_tiles = {}, {}, {}, {}, {}, {}
        dt_banks, s1_banks, s2_banks = {}, {}, {}

        def transpose_distances(u):
            dt_banks[u] = []
            for r in range(TILES):
                d_words = d_units[u][:, r, :].bitcast(F32)
                dt_ps = psum.tile([P, D_PASSES, 2, P], F32, tag="dt", bufs=DT_BUFS, name="dt_ps")
                dt_banks[u].append(dt_ps)
                for g in range(D_PASSES):
                    for e in range(2):
                        nc.tensor.transpose(
                            out=dt_ps[:, g, e, :],
                            in_=d_words[:, 256 * g + e : 256 * (g + 1) : 2],
                            identity=ident_f32[:],
                        )
                if r == 0:
                    d_grouped[u] = work.tile([P, D_PASSES, TILES, P, PACK], BF16, align_bytes=64, name="d_grouped")
                copy_distances(u, r)

        def copy_distances(u, r):
            nc.scalar.copy(
                out=d_grouped[u][:, :, r].bitcast(F32), in_=dt_banks[u][r][:].rearrange("p g e c -> p g c e")
            )

        def quantise_distances(u):
            words = work.tile([P, D_PASSES, PAIRS], U32, align_bytes=64, name="d_words")
            plane = work.tile([P, D_PASSES, PAIRS], U8, align_bytes=64, name="d_plane")
            nc.vector.quantize_mx(
                out=words[:].rearrange("p g c -> p (g c)").bitcast(FP8X4),
                scales=plane[:].rearrange("p g c -> p (g c)"),
                in_=d_grouped[u][:].rearrange("p g r c t -> p (g r c t)"),
            )
            d_codes[u] = (words, plane)

        def first_matmul(u):
            words, plane = d_codes[u]
            s1_banks[u] = []
            for half in range(PACK // 2):
                s1_ps = psum.tile([P, 2, PAIRS], F32, tag="s1", bufs=S1_BUFS, name="s1_ps")
                s1_banks[u].append(s1_ps)
                for e in range(2):
                    t = 2 * half + e
                    for g in range(D_PASSES):
                        nc.tensor.matmul_mx(
                            out=s1_ps[:, e, :],
                            lhsT=wdf_words[:, g, t * P : (t + 1) * P].bitcast(FP8X4),
                            lhsT_scale=wdf_planes[:, g, t * P : (t + 1) * P],
                            rhs=words[:, g, :].bitcast(FP8X4),
                            rhs_scale=plane[:, g, :],
                            start=(g == 0),
                            stop=(g == D_PASSES - 1),
                        )

        def gate(u):
            gated = work.tile([P, PACK, PAIRS], BF16, name="gated")
            gated_tiles[u] = gated
            jb = TILES * MOLS
            for t in range(PACK):
                nc.vector.scalar_tensor_tensor(
                    out=gated[:, t, :].rearrange("p (q i) -> p q i", i=ATOMS),
                    in0=s1_banks[u][t // 2][:, t % 2, :].rearrange("p (q i) -> p q i", i=ATOMS),
                    scalar=bdf_x[:, t : t + 1],
                    in1=atom_x[:, t, u * jb : (u + 1) * jb].unsqueeze(2).to_broadcast([P, jb, ATOMS]),
                    op0=ADD,
                    op1=MULT,
                )

        def gate_runs(u, runs):
            gated = work.tile([P, PACK, PAIRS], BF16, name="gated")
            gated_tiles[u] = gated
            jb = TILES * MOLS
            for t in runs:
                nc.vector.scalar_tensor_tensor(
                    out=gated[:, t, :].rearrange("p (q i) -> p q i", i=ATOMS),
                    in0=s1_banks[u][t // 2][:, t % 2, :].rearrange("p (q i) -> p q i", i=ATOMS),
                    scalar=bdf_x[:, t : t + 1],
                    in1=atom_x[:, t, u * jb : (u + 1) * jb].unsqueeze(2).to_broadcast([P, jb, ATOMS]),
                    op0=ADD,
                    op1=MULT,
                )

        def gate_scalar(u, t):
            jb = TILES * MOLS
            for q in range(jb):
                c = u * jb + q
                nc.scalar.activation(
                    out=gated_tiles[u][:, t, q * ATOMS : (q + 1) * ATOMS],
                    in_=s1_banks[u][t // 2][:, t % 2, q * ATOMS : (q + 1) * ATOMS],
                    func=IDENTITY,
                    scale=atom_x[:, t, c : c + 1],
                    bias=shift_x[:, t, c : c + 1],
                )

        def make_shift(t):
            nc.vector.tensor_scalar(out=shift_x[:, t, :], in0=atom_x[:, t, :], scalar1=bdf_x[:, t : t + 1], scalar2=None, op0=MULT)

        shift_x = consts.tile([P, PACK, ATOMS * MOLS], F32)

        def group_gated(u):
            grouped = work.tile([P, PAIRS, PACK], BF16, align_bytes=64, name="g_grouped")
            g_grouped[u] = grouped
            nc.scalar.copy(
                out=grouped[:].rearrange("p (c i) t -> p c t i", i=4),
                in_=gated_tiles[u][:].rearrange("p t (c i) -> p c t i", i=4),
            )

        def first_matmul_tile(u, r):
            words, plane = d_codes[u]
            s1_ps = psum.tile([P, PACK, P], F32, tag="s1", bufs=S1_BUFS, name="s1_ps")
            s1_banks[u, r] = s1_ps
            c = slice(r * P, (r + 1) * P)
            for t in range(PACK):
                for g in range(D_PASSES):
                    nc.tensor.matmul_mx(
                        out=s1_ps[:, t, :],
                        lhsT=wdf_words[:, g, t * P : (t + 1) * P].bitcast(FP8X4),
                        lhsT_scale=wdf_planes[:, g, t * P : (t + 1) * P],
                        rhs=words[:, g, c].bitcast(FP8X4),
                        rhs_scale=plane[:, g, c],
                        start=(g == 0),
                        stop=(g == D_PASSES - 1),
                    )

        def gate_tile(u, r):
            gated = work.tile([P, PACK, P], BF16, name="gated_t")
            gated_tiles[u, r] = gated
            j = u * TILES + r
            for t in range(PACK):
                nc.vector.scalar_tensor_tensor(
                    out=gated[:, t, :].rearrange("p (q i) -> p q i", i=ATOMS),
                    in0=s1_banks[u, r][:, t, :].rearrange("p (q i) -> p q i", i=ATOMS),
                    scalar=bdf_x[:, t : t + 1],
                    in1=atom_x[:, t, j * MOLS : (j + 1) * MOLS].unsqueeze(2).to_broadcast([P, MOLS, ATOMS]),
                    op0=ADD,
                    op1=MULT,
                )

        def group_tile(u, r):
            grouped = work.tile([P, P, PACK], BF16, align_bytes=64, name="g_grouped_t")
            g_grouped[u, r] = grouped
            nc.scalar.copy(
                out=grouped[:].rearrange("p (c i) t -> p c t i", i=4),
                in_=gated_tiles[u, r][:].rearrange("p t (c i) -> p c t i", i=4),
            )

        def quantise_tile(u, r):
            words = work.tile([P, P], U32, align_bytes=64, name="g_words_t")
            plane = work.tile([P, P], U8, align_bytes=64, name="g_plane_t")
            nc.vector.quantize_mx(
                out=words[:].bitcast(FP8X4), scales=plane[:], in_=g_grouped[u, r][:].rearrange("p c t -> p (c t)")
            )
            g_codes[u, r] = (words, plane)

        def second_matmul_tile(u, r):
            words, plane = g_codes[u, r]
            s2_ps = psum.tile([P, NF], F32, tag="s2", bufs=S2_BUFS, name="s2_ps")
            s2_banks.setdefault(u, []).append(s2_ps)
            nc.tensor.matmul_mx(
                out=s2_ps[:],
                lhsT=words[:].bitcast(FP8X4),
                lhsT_scale=plane[:],
                rhs=wfc_words[:].bitcast(FP8X4),
                rhs_scale=w_planes[:, D_PASSES, :],
                start=True,
                stop=True,
            )

        def squash_tile(u, r):
            if r == 0:
                th_tiles[u] = work.tile([P, TILES, NF], F32, name="th_sb")
            j = u * TILES + r
            nc.scalar.activation(
                out=th_tiles[u][:, r, :], in_=s2_banks[u][r][:], func=TANH, scale=mask_f32[:, j : j + 1]
            )

        def open_gpsimd(u):
            grouped = work.tile([P, PAIRS, PACK], BF16, align_bytes=64, name="g_grouped")
            g_grouped[u] = grouped
            nc.vector.memset(grouped[:, 0, :], 0.0)

        def group_g(u):
            grouped = g_grouped[u]
            nc.gpsimd.tensor_scalar(
                out=grouped[:].rearrange("p (c i) t -> p c t i", i=4),
                in0=gated_tiles[u][:].rearrange("p t (c i) -> p c t i", i=4),
                scalar1=1.0,
                scalar2=0.0,
                op0=MULT,
                op1=ADD,
            )

        def split_group(u, pairs, engine):
            dst = g_grouped[u][:, pairs, :].rearrange("p (c i) t -> p c t i", i=4)
            src = gated_tiles[u][:, :, pairs].rearrange("p t (c i) -> p c t i", i=4)
            if engine == "gpsimd":
                nc.gpsimd.tensor_scalar(out=dst, in0=src, scalar1=1.0, scalar2=0.0, op0=MULT, op1=ADD)
            else:
                nc.scalar.copy(out=dst, in_=src)

        def group_v(u):
            grouped = work.tile([P, PAIRS, PACK], BF16, align_bytes=64, name="g_grouped")
            g_grouped[u] = grouped
            nc.vector.tensor_copy(
                out=grouped[:].rearrange("p (c i) t -> p c t i", i=4),
                in_=gated_tiles[u][:].rearrange("p t (c i) -> p c t i", i=4),
            )

        def quantise_gated(u):
            words = work.tile([P, PAIRS], U32, align_bytes=64, name="g_words")
            plane = work.tile([P, PAIRS], U8, align_bytes=64, name="g_plane")
            nc.vector.quantize_mx(
                out=words[:].bitcast(FP8X4),
                scales=plane[:],
                in_=g_grouped[u][:].rearrange("p c t -> p (c t)"),
            )
            g_codes[u] = (words, plane)

        def second_matmul(u):
            words, plane = g_codes[u]
            s2_banks[u] = []
            for r in range(TILES):
                s2_ps = psum.tile([P, NF], F32, tag="s2", bufs=S2_BUFS, name="s2_ps")
                s2_banks[u].append(s2_ps)
                nc.tensor.matmul_mx(
                    out=s2_ps[:],
                    lhsT=words[:, r * P : (r + 1) * P].bitcast(FP8X4),
                    lhsT_scale=plane[:, r * P : (r + 1) * P],
                    rhs=wfc_words[:].bitcast(FP8X4),
                    rhs_scale=w_planes[:, D_PASSES, :],
                    start=True,
                    stop=True,
                )

        def squash(u):
            th_sb = sums if u == 0 else work.tile([P, TILES, NF], F32, name="th_sb")
            th_tiles[u] = th_sb
            for r in range(TILES):
                j = u * TILES + r
                nc.scalar.activation(out=th_sb[:, r, :], in_=s2_banks[u][r][:], func=TANH, scale=mask_f32[:, j : j + 1])

        t_sum = {}

        def start_tensor_sum0():
            acc = psum.tile([P, F_CHUNKS, P], F32, tag="dt", bufs=DT_BUFS, name="acc_ps")
            tiles = [(u, r) for u in T_UNITS for r in range(TILES)]
            for c in range(F_CHUNKS):
                for n, (u, r) in enumerate(tiles):
                    nc.tensor.matmul(
                        out=acc[:, c, :],
                        lhsT=th_tiles[u][:, r, c * P : (c + 1) * P],
                        rhs=ident_f32[:],
                        is_transpose=True,
                        start=(n == 0),
                        stop=(n == len(tiles) - 1),
                    )
            t_sum["acc"] = acc

        def start_tensor_sum1():
            acc_sb = consts.tile([P, F_CHUNKS, P], F32, name="acc_sb")
            nc.scalar.copy(out=acc_sb[:], in_=t_sum["acc"][:])
            t_sum["sb"] = acc_sb

        def tensor_add(u):
            first = u == T_UNITS[0]
            last = u == T_UNITS[-1]
            if first:
                t_sum["acc"] = psum.tile([P, F_CHUNKS, P], F32, tag="acc", bufs=1, name="acc_ps")
            acc = t_sum["acc"]
            for r in range(T_FROM, TILES):
                for c in range(F_CHUNKS):
                    nc.tensor.matmul(
                        out=acc[:, c, :],
                        lhsT=th_tiles[u][:, r, c * P : (c + 1) * P],
                        rhs=ident_f32[:],
                        is_transpose=True,
                        start=(first and r == T_FROM and c == 0),
                        stop=(last and r == TILES - 1 and c == F_CHUNKS - 1),
                    )

        def turn_tensor_sum():
            back = psum.tile([P, NF], F32, tag="dt", bufs=DT_BUFS, name="back_ps")
            for c in range(F_CHUNKS):
                nc.tensor.transpose(out=back[:, c * P : (c + 1) * P], in_=t_sum["sb"][:, c, :], identity=ident_f32[:])
            t_sum["back"] = back

        def halves():
            return [slice(h * NF // 2, (h + 1) * NF // 2) for h in range(2)]

        def join_sums():
            for h in halves():
                nc.vector.tensor_tensor(out=sums[:, 0, h], in0=sums[:, 0, h], in1=sums[:, 1, h], op=ADD)

        def add_tensor_sum():
            for h in halves():
                nc.vector.tensor_tensor(out=sums[:, 0, h], in0=sums[:, 0, h], in1=t_sum["back"][:, h], op=ADD)

        def add_tile(u, r):
            for h in halves():
                nc.vector.tensor_tensor(out=sums[:, 0, h], in0=sums[:, 0, h], in1=th_tiles[u][:, r, h], op=ADD)

        def add_tiles(u):
            for r in range(TILES):
                add_tile(u, r)

        def add_up(u):
            if u in T_UNITS:
                for r in range(T_FROM):
                    nc.vector.tensor_tensor(out=sums[:, r, :], in0=sums[:, r, :], in1=th_tiles[u][:, r, :], op=ADD)
                return
            if u == 0:
                nc.vector.tensor_tensor(out=sums[:, 0, :], in0=sums[:, 0, :], in1=a_sb[:], op=ADD)
            elif u in G_UNITS:
                flat = sums[:].rearrange("p r f -> p (r f)")[:, 0 : TILES * NF - G_COLS]
                new = th_tiles[u][:].rearrange("p r f -> p (r f)")[:, 0 : TILES * NF - G_COLS]
                nc.vector.tensor_tensor(out=flat, in0=flat, in1=new, op=ADD)
            else:
                nc.vector.tensor_tensor(out=sums[:], in0=sums[:], in1=th_tiles[u][:], op=ADD)

        def add_gpsimd(u):
            mine = sums[:, 1, NF - G_COLS : NF]
            nc.gpsimd.tensor_tensor(out=mine, in0=mine, in1=th_tiles[u][:, 1, NF - G_COLS : NF], op=ADD)

        def live(u):
            return 0 <= u < UNITS

        cast_biases()
        keep_warm(12)
        transpose_distances(0)
        quantise_distances(0)
        transpose_atoms()
        keep_warm(6)
        transpose_distances(1)
        keep_warm(6)
        reorder_words()
        reorder_scales()
        quantise_distances(1)
        atom_layer()
        add_atom_bias()
        transpose_distances(2)
        first_matmul(0)
        gate(0)
        quantise_distances(2)
        first_matmul(1)
        gate(1)
        group_gated(0)
        quantise_gated(0)
        cast_mask()
        for k in range(3, UNITS):
            if k - 2 in range(1, 14):
                open_gpsimd(k - 2)
            if live(k - 0):
                transpose_distances(k - 0)
            if k - 4 in T_UNITS:
                tensor_add(k - 4)
            if live(k - 0):
                quantise_distances(k - 0)
            if k - 2 in range(1, 14):
                split_group(k - 2, slice(0, 64), "gpsimd")
            if k - 4 in G_UNITS:
                add_gpsimd(k - 4)
            first_matmul(k - 1)
            gate(k - 1)
            if k - 2 in range(1, 14):
                split_group(k - 2, slice(64, PAIRS), "scalar")
            else:
                group_gated(k - 2)
            quantise_gated(k - 2)
            if live(k - 3):
                second_matmul(k - 3)
            if live(k - 3):
                squash(k - 3)
            if live(k - 3) and k - 3 <= 12:
                add_up(k - 3)

        first_matmul(15)
        gate(15)
        group_gated(14)
        quantise_gated(14)
        second_matmul(13)
        squash(13)
        group_gated(15)
        add_up(13)
        quantise_gated(15)
        second_matmul(14)
        squash(14)
        join_sums()
        second_matmul(15)
        squash(15)
        add_tiles(14)
        add_tiles(15)

        for h in halves():
            nc.sync.dma_start(out=out.rearrange("b i f -> (b i) f")[:, h], in_=sums[:, 0, h])
